import numpy as np
import ml_dtypes


def mxq(x, axis, fmt="e4m3"):
    dtype, down = {"e4m3": (ml_dtypes.float8_e4m3fn, 7), "e5m2": (ml_dtypes.float8_e5m2, 14)}[fmt]
    v = np.moveaxis(np.asarray(x, np.float32).astype(ml_dtypes.bfloat16).astype(np.float64), axis, -1)
    blocks = v.reshape(v.shape[:-1] + (-1, 32))
    amax = np.abs(blocks).max(-1, keepdims=True)
    byte = np.maximum(np.where(amax > 0, np.frexp(amax)[1] - 1 + 127, 0) - down, 1)
    scale = np.exp2(byte - 127.0)
    codes = (blocks / scale).astype(np.float32).astype(dtype).astype(np.float64)
    return np.moveaxis((codes * scale).reshape(v.shape), -1, axis)


WIDE = False


def mx_kscale(k):
    if not WIDE:
        return np.ones(k)
    levels = np.array([10, -10, 5, -5, 0])
    if k % 512:
        return np.exp2(np.random.permutation(np.resize(levels, k // 32))).repeat(32)
    a = np.empty((k // 512, 16))
    for p in range(k // 512):
        a[p, :8] = np.random.permutation(np.resize(levels, 8))
        for g in range(8):
            far = levels[np.abs(levels - a[p, g]) >= 10]
            a[p, g + 8] = far[np.random.randint(len(far))]
    return np.exp2(a.ravel()).repeat(32)


BF16 = ml_dtypes.bfloat16


def bf(x):
    return np.asarray(x, np.float32).astype(BF16)


def f64(x):
    return np.asarray(x).astype(np.float64)


B, L, S, D, DA, H, MLP = 2, 3, 1024, 512, 1024, 16, 4096
EPS = 1e-5


def layer_norm(u, g, b):
    mu = u.mean(-1, keepdims=True)
    var = ((u - mu) ** 2).mean(-1, keepdims=True)
    return (u - mu) / np.sqrt(var + EPS) * g + b


def grn(st, stq, W, b, g, be):
    w = np.maximum((stq @ mxq(f64(W), 0, "e4m3")).reshape(B, L, S, D) + f64(b), 0.0)
    n = layer_norm(st, f64(g), f64(be))
    return (w + n).sum(1)


def setup_inputs():
    s = mx_kscale(D)
    r = np.random.standard_normal
    return {"layer_outputs": bf(r((B, L, S, D)) * s),
            "grn_q_W": bf(r((D, D)) / np.sqrt(D) / s[:, None]), "grn_q_b": bf(r(D) * 0.2), "grn_q_g": bf(1.0 + 0.1 * r(D)), "grn_q_be": bf(r(D) * 0.1),
            "grn_k_W": bf(r((D, D)) / np.sqrt(D) / s[:, None]), "grn_k_b": bf(r(D) * 0.2), "grn_k_g": bf(1.0 + 0.1 * r(D)), "grn_k_be": bf(r(D) * 0.1),
            "grn_v_W": bf(r((D, D)) / np.sqrt(D) / s[:, None]), "grn_v_b": bf(r(D) * 0.2), "grn_v_g": bf(1.0 + 0.1 * r(D)), "grn_v_be": bf(r(D) * 0.1)}


def reference(layer_outputs, grn_q_W, grn_q_b, grn_q_g, grn_q_be, grn_k_W, grn_k_b, grn_k_g, grn_k_be, grn_v_W, grn_v_b, grn_v_g, grn_v_be):
    st = f64(layer_outputs)
    stq = mxq(st.reshape(B * L * S, D), 1, "e4m3")
    q = grn(st, stq, grn_q_W, grn_q_b, grn_q_g, grn_q_be)
    k = grn(st, stq, grn_k_W, grn_k_b, grn_k_g, grn_k_be)
    v = grn(st, stq, grn_v_W, grn_v_b, grn_v_g, grn_v_be)
    return q, k, v

@@ -1,0 +1,308 @@
+from contextlib import ExitStack
+
+import concourse.mybir as mybir
+from concourse.masks import make_identity
+
+F32 = mybir.dt.float32
+BF16 = mybir.dt.bfloat16
+U32 = mybir.dt.uint32
+U8 = mybir.dt.uint8
+FP8X4 = mybir.dt.float8_e4m3fn_x4
+ALU = mybir.AluOpType
+ACT = mybir.ActivationFunctionType
+
+BATCH, LAYERS, SEQ, D = 2, 3, 1024, 512
+EPS = 1e-5
+P = 128
+PACK = 4
+TILES = 4
+HALVES = SEQ // (P * TILES)
+GROUPS = BATCH * HALVES
+BLOCKS = D // P
+KINDS = 3
+PER_GROUP = BLOCKS * LAYERS
+STEPS = GROUPS * PER_GROUP
+
+LEAD_SEED = 3
+LEAD_NT = 6
+LEAD_SCALE = 19
+LEAD_RSTD = 22
+LEAD_STD = 23
+LEAD_STATS = 24
+LEAD_QUANTISE = 11
+LEAD_XT = 12
+LEAD_WEIGHTS = 14
+LEAD_CONSTANTS = 8
+LAG_BACK = 3
+
+FLOPS = 2 * BATCH * LAYERS * SEQ * D * KINDS * D
+
+
+def tile_dcadecoderblock_pa_t_kernel(
+    tc,
+    layer_outputs,
+    grn_q_W, grn_q_b, grn_q_g, grn_q_be,
+    grn_k_W, grn_k_b, grn_k_g, grn_k_be,
+    grn_v_W, grn_v_b, grn_v_g, grn_v_be,
+    out_0, out_1, out_2,
+):
+    nc = tc.nc
+    weights = [grn_q_W, grn_k_W, grn_v_W]
+    vectors = [grn_q_b, grn_q_g, grn_q_be, grn_k_b, grn_k_g, grn_k_be, grn_v_b, grn_v_g, grn_v_be]
+    outs = [out_0, out_1, out_2]
+
+    with ExitStack() as stack:
+        stack.enter_context(tc.manual_schedule())
+        keep = stack.enter_context(tc.tile_pool(name="keep", bufs=1))
+        stage = stack.enter_context(tc.tile_pool(name="stage", bufs=2))
+        small = stack.enter_context(tc.tile_pool(name="small", bufs=4))
+        psum = stack.enter_context(tc.psum_pool(name="psum", bufs=1))
+
+        def rows_of_group(dram, g):
+            return dram[g // HALVES].rearrange("(p h i) f -> p h i f", h=HALVES, i=TILES)[:, g % HALVES]
+
+        x_sb = {}
+
+        def load_group(g):
+            for l in range(LAYERS):
+                x = keep.tile([P, TILES, D], BF16, name="x%d_%d" % (g, l))
+                nc.sync.dma_start(out=x[:], in_=rows_of_group(layer_outputs[:, l], g))
+                x_sb[(g, l)] = x
+
+        load_group(0)
+        w_raw = []
+        for t in range(KINDS):
+            raw = keep.tile([P, PACK, D], BF16, name="w_raw%d" % t)
+            nc.sync.dma_start(out=raw[:], in_=weights[t].rearrange("(p j) c -> p j c", j=PACK))
+            w_raw.append(raw)
+        vec_rows = keep.tile([P, P], BF16, name="vec_rows")
+        nc.vector.memset(vec_rows[:], 0.0)
+        for n, vec in enumerate(vectors):
+            nc.sync.dma_start(
+                out=vec_rows[BLOCKS * n : BLOCKS * n + BLOCKS, :],
+                in_=vec.rearrange("(j p) -> j p", p=P),
+            )
+        for g in range(1, GROUPS):
+            load_group(g)
+
+        ident_f = keep.tile([P, P], F32, name="ident_f")
+        make_identity(nc, ident_f[:])
+        ident_b = keep.tile([P, P], BF16, name="ident_b")
+        make_identity(nc, ident_b[:])
+        eps = keep.tile([P, 1], F32, name="eps")
+        nc.vector.memset(eps[:], EPS)
+
+        vec_cols = keep.tile([P, KINDS, 3, BLOCKS], F32, name="vec_cols")
+        bias = vec_cols[:, :, 0, :]
+        gain = vec_cols[:, :, 1, :]
+        shift = vec_cols[:, :, 2, :]
+        neg_bias = keep.tile([P, KINDS, BLOCKS], F32, name="neg_bias")
+        rest = keep.tile([P, KINDS, BLOCKS], F32, name="rest")
+
+        def split(index):
+            g, within = divmod(index, PER_GROUP)
+            a, c = divmod(within, LAYERS)
+            return g, a, c
+
+        def constants(index):
+            if index != 0:
+                return
+            vec_ps = psum.tile([P, P], BF16, tag="xt", name="vec_ps")
+            nc.tensor.transpose(vec_ps[:], vec_rows[:], ident_b[:])
+            nc.vector.tensor_copy(
+                out=vec_cols[:].rearrange("p t v j -> p (t v j)"), in_=vec_ps[:, 0 : KINDS * 3 * BLOCKS]
+            )
+            nc.vector.tensor_scalar_mul(out=neg_bias[:], in0=bias, scalar1=-1.0)
+            nc.vector.tensor_add(out=rest[:], in0=bias, in1=shift)
+            nc.vector.tensor_scalar_mul(out=rest[:], in0=rest[:], scalar1=3.0)
+
+        w_grouped = {}
+        w_codes = {}
+        w_scales = {}
+
+        def regroup_weight(t):
+            if not 0 <= t < KINDS:
+                return
+            grouped = stage.tile([P, D, PACK], BF16, align_bytes=64, name="w_grouped")
+            nc.scalar.copy(
+                out=grouped[:].rearrange("p (c i) t -> p c t i", i=4),
+                in_=w_raw[t][:].rearrange("p t (c i) -> p c t i", i=4),
+            )
+            w_grouped[t] = grouped
+
+        def quantise_weight(t):
+            if not 0 <= t < KINDS:
+                return
+            w_codes[t] = keep.tile([P, D], U32, align_bytes=64, name="w_codes%d" % t)
+            w_scales[t] = keep.tile([P, D], U8, align_bytes=64, name="w_scales%d" % t)
+            nc.vector.quantize_mx(
+                out=w_codes[t][:].bitcast(FP8X4),
+                scales=w_scales[t][:],
+                in_=w_grouped[t][:].rearrange("p c t -> p (c t)"),
+            )
+
+        x_grouped = {}
+        x_codes = {}
+        x_scales = {}
+
+        def transpose_x(index):
+            if not 0 <= index < STEPS:
+                return
+            g, i, l = split(index)
+            words = x_sb[(g, l)][:].bitcast(F32)
+            xt = psum.tile([P, 2, P], F32, tag="xt", name="xt")
+            for u in range(2):
+                nc.tensor.transpose(xt[:, u, :], words[:, i, u : 2 * P : 2], ident_f[:])
+            grouped = stage.tile([P, P, PACK], BF16, align_bytes=64, bufs=3, name="x_grouped")
+            nc.scalar.copy(out=grouped[:].bitcast(F32), in_=xt[:].rearrange("p u r -> p r u"))
+            x_grouped[index] = grouped
+
+        def quantise_x(index):
+            if not 0 <= index < STEPS:
+                return
+            g, i, l = split(index)
+            if i == 0:
+                x_codes[(g, l)] = stage.tile([P, TILES * P], U32, align_bytes=64, bufs=6, name="x_codes")
+                x_scales[(g, l)] = stage.tile([P, TILES * P], U8, align_bytes=64, bufs=6, name="x_scales")
+            nc.vector.quantize_mx(
+                out=x_codes[(g, l)][:, P * i : P * i + P].bitcast(FP8X4),
+                scales=x_scales[(g, l)][:, P * i : P * i + P],
+                in_=x_grouped[index][:].rearrange("p r t -> p (r t)"),
+            )
+
+        stats = {}
+        mean_var = {}
+        std = {}
+        rstd = {}
+        offset = {}
+        normed = {}
+
+        def statistics(index):
+            if not 0 <= index < STEPS:
+                return
+            g, i, l = split(index)
+            if l == 0:
+                stats[(g, i)] = small.tile([P, LAYERS, 6], F32, name="stats")
+            nc.vector.bn_stats(out=stats[(g, i)][:, l, :], in_=x_sb[(g, l)][:, i, :])
+
+        def aggregate(index):
+            if not 0 <= index < STEPS:
+                return
+            g, i, l = split(index)
+            if l == 0:
+                mean_var[(g, i)] = small.tile([P, LAYERS, 2], F32, name="mean_var")
+            nc.vector.bn_aggr(out=mean_var[(g, i)][:, l, :], in_=stats[(g, i)][:, l, :])
+
+        def deviation(index):
+            if not 0 <= index < STEPS:
+                return
+            g, i, l = split(index)
+            if l == LAYERS - 1:
+                std[(g, i)] = small.tile([P, LAYERS], F32, name="std")
+                nc.scalar.activation(
+                    out=std[(g, i)][:], in_=mean_var[(g, i)][:, :, 1], func=ACT.Sqrt, bias=eps[:], scale=1.0
+                )
+
+        def reciprocal(index):
+            if not 0 <= index < STEPS:
+                return
+            g, i, l = split(index)
+            if l == LAYERS - 1:
+                rstd[(g, i)] = small.tile([P, LAYERS], F32, name="rstd")
+                nc.vector.reciprocal(out=rstd[(g, i)][:], in_=std[(g, i)][:])
+                offset[(g, i)] = small.tile([P, LAYERS], F32, name="offset")
+                nc.vector.scalar_tensor_tensor(
+                    out=offset[(g, i)][:], in0=mean_var[(g, i)][:, :, 0], scalar=-1.0, in1=rstd[(g, i)][:],
+                    op0=ALU.mult, op1=ALU.mult,
+                )
+
+        def scale(index):
+            if not 0 <= index < STEPS:
+                return
+            g, i, l = split(index)
+            y = stage.tile([P, D], F32, bufs=2 * PER_GROUP, name="normed")
+            nc.gpsimd.tensor_scalar(
+                out=y[:], in0=x_sb[(g, l)][:, i, :],
+                scalar1=rstd[(g, i)][:, l : l + 1], scalar2=offset[(g, i)][:, l : l + 1],
+                op0=ALU.mult, op1=ALU.add,
+            )
+            normed[(g, i, l)] = y
+
+        nt = {}
+        acc = {}
+
+        def transpose_normed(index):
+            if not 0 <= index < STEPS:
+                return
+            g, j, third = split(index)
+            if third == 0:
+                nt[(g, j)] = psum.tile([P, TILES * P], F32, tag="nt", bufs=2, name="nt")
+            for n in range(TILES * third, TILES * third + TILES):
+                i, l = divmod(n, LAYERS)
+                nc.tensor.matmul(
+                    out=nt[(g, j)][:, P * i : P * i + P],
+                    lhsT=normed[(g, i, l)][:, P * j : P * j + P],
+                    rhs=ident_f[:],
+                    is_transpose=True,
+                    start=(l == 0),
+                    stop=(l == LAYERS - 1),
+                )
+
+        def seed(index):
+            if not 0 <= index < STEPS:
+                return
+            g, j, t = split(index)
+            a = stage.tile([P, TILES * P], F32, bufs=10, name="acc")
+            nc.scalar.activation(
+                out=a[:], in_=nt[(g, j)][:], func=ACT.Identity,
+                scale=gain[:, t, j : j + 1], bias=rest[:, t, j : j + 1],
+            )
+            acc[(g, t, j)] = a
+
+        def products(index):
+            if not 0 <= index < STEPS:
+                return
+            g, j, l = split(index)
+            cols = slice(P * j, P * j + P)
+            for t in range(KINDS):
+                prod = psum.tile([P, TILES * P], F32, tag="prod", bufs=3, name="prod")
+                nc.tensor.matmul_mx(
+                    out=prod[:],
+                    lhsT=w_codes[t][:, cols].bitcast(FP8X4),
+                    lhsT_scale=w_scales[t][:, cols],
+                    rhs=x_codes[(g, l)][:].bitcast(FP8X4),
+                    rhs_scale=x_scales[(g, l)][:],
+                    start=True,
+                    stop=True,
+                )
+                nc.vector.scalar_tensor_tensor(
+                    out=acc[(g, t, j)][:], in0=prod[:], scalar=neg_bias[:, t, j : j + 1],
+                    in1=acc[(g, t, j)][:], op0=ALU.max, op1=ALU.add,
+                )
+
+        def back(index):
+            if not 0 <= index < STEPS:
+                return
+            g, j, t = split(index)
+            turned = psum.tile([P, TILES, P], F32, tag="back", bufs=2, name="turned")
+            for i in range(TILES):
+                nc.tensor.transpose(turned[:, i, :], acc[(g, t, j)][:, P * i : P * i + P], ident_f[:])
+            result = stage.tile([P, TILES, P], F32, bufs=4, name="result")
+            nc.scalar.copy(out=result[:], in_=turned[:])
+            nc.sync.dma_start(out=rows_of_group(outs[t], g)[:, :, P * j : P * j + P], in_=result[:])
+
+        for step in range(-LEAD_STATS, STEPS + LAG_BACK):
+            products(step)
+            deviation(step + LEAD_STD)
+            seed(step + LEAD_SEED)
+            back(step - LAG_BACK)
+            transpose_normed(step + LEAD_NT)
+            transpose_x(step + LEAD_XT)
+            regroup_weight(step + LEAD_WEIGHTS)
+            constants(step + LEAD_CONSTANTS)
+            statistics(step + LEAD_STATS)
+            quantise_x(step + LEAD_QUANTISE)
+            quantise_weight(step + LEAD_WEIGHTS - 1)
+            aggregate(step + LEAD_STATS)
+            reciprocal(step + LEAD_RSTD)
+            scale(step + LEAD_SCALE)

@@ -20,20 +20,16 @@ HALVES = SEQ // (P * TILES)
 GROUPS = BATCH * HALVES
 BLOCKS = D // P
 KINDS = 3
-PER_GROUP = BLOCKS * LAYERS
-STEPS = GROUPS * PER_GROUP
 
-LEAD_SEED = 3
-LEAD_NT = 6
-LEAD_SCALE = 19
-LEAD_RSTD = 22
-LEAD_STD = 23
-LEAD_STATS = 24
-LEAD_QUANTISE = 11
-LEAD_XT = 12
-LEAD_WEIGHTS = 14
-LEAD_CONSTANTS = 8
-LAG_BACK = 3
+UNITS = GROUPS * BLOCKS * KINDS
+PHASES = UNITS // 2
+ROW_TILES = GROUPS * LAYERS * TILES
+
+LEAD_FILL = 2
+LEAD_XT = 7
+LEAD_QUANTISE = 6
+LEAD_SCALE = 7
+LEAD_STATS = 9
 
 FLOPS = 2 * BATCH * LAYERS * SEQ * D * KINDS * D
 
@@ -63,18 +59,21 @@ def tile_dcadecoderblock_pa_t_kernel(
 
         x_sb = {}
 
-        def load_group(g):
-            for l in range(LAYERS):
-                x = keep.tile([P, TILES, D], BF16, name="x%d_%d" % (g, l))
-                nc.sync.dma_start(out=x[:], in_=rows_of_group(layer_outputs[:, l], g))
-                x_sb[(g, l)] = x
+        def load_x(g, l):
+            x = keep.tile([P, TILES, D], BF16, name="x%d_%d" % (g, l))
+            nc.sync.dma_start(out=x[:], in_=rows_of_group(layer_outputs[:, l], g))
+            x_sb[(g, l)] = x
 
-        load_group(0)
-        w_raw = []
-        for t in range(KINDS):
+        w_raw = {}
+
+        def load_w(t):
             raw = keep.tile([P, PACK, D], BF16, name="w_raw%d" % t)
             nc.sync.dma_start(out=raw[:], in_=weights[t].rearrange("(p j) c -> p j c", j=PACK))
-            w_raw.append(raw)
+            w_raw[t] = raw
+
+        for n in range(LAYERS):
+            load_x(0, n)
+            load_w(n)
         vec_rows = keep.tile([P, P], BF16, name="vec_rows")
         nc.vector.memset(vec_rows[:], 0.0)
         for n, vec in enumerate(vectors):
@@ -83,7 +82,8 @@ def tile_dcadecoderblock_pa_t_kernel(
                 in_=vec.rearrange("(j p) -> j p", p=P),
             )
         for g in range(1, GROUPS):
-            load_group(g)
+            for l in range(LAYERS):
+                load_x(g, l)
 
         ident_f = keep.tile([P, P], F32, name="ident_f")
         make_identity(nc, ident_f[:])
@@ -97,42 +97,51 @@ def tile_dcadecoderblock_pa_t_kernel(
         gain = vec_cols[:, :, 1, :]
         shift = vec_cols[:, :, 2, :]
         neg_bias = keep.tile([P, KINDS, BLOCKS], F32, name="neg_bias")
-        rest = keep.tile([P, KINDS, BLOCKS], F32, name="rest")
+        rest2 = keep.tile([P, KINDS, BLOCKS], F32, name="rest2")
+        rest3 = keep.tile([P, KINDS, BLOCKS], F32, name="rest3")
 
-        def split(index):
-            g, within = divmod(index, PER_GROUP)
-            a, c = divmod(within, LAYERS)
-            return g, a, c
+        def split_unit(u):
+            g, within = divmod(u, BLOCKS * KINDS)
+            j, t = divmod(within, KINDS)
+            return g, j, t
 
-        def constants(index):
-            if index != 0:
-                return
+        def split_tile(s):
+            g, within = divmod(s, LAYERS * TILES)
+            l, i = divmod(within, TILES)
+            return g, l, i
+
+        def on_scalar(u):
+            return u % 2 == 0
+
+        def constants():
             vec_ps = psum.tile([P, P], BF16, tag="xt", name="vec_ps")
             nc.tensor.transpose(vec_ps[:], vec_rows[:], ident_b[:])
             nc.vector.tensor_copy(
                 out=vec_cols[:].rearrange("p t v j -> p (t v j)"), in_=vec_ps[:, 0 : KINDS * 3 * BLOCKS]
             )
             nc.vector.tensor_scalar_mul(out=neg_bias[:], in0=bias, scalar1=-1.0)
-            nc.vector.tensor_add(out=rest[:], in0=bias, in1=shift)
-            nc.vector.tensor_scalar_mul(out=rest[:], in0=rest[:], scalar1=3.0)
+            nc.vector.tensor_scalar_mul(out=rest2[:], in0=shift, scalar1=3.0)
+            nc.vector.scalar_tensor_tensor(
+                out=rest3[:], in0=bias, scalar=3.0, in1=rest2[:], op0=ALU.mult, op1=ALU.add
+            )
+            nc.vector.scalar_tensor_tensor(
+                out=rest2[:], in0=bias, scalar=2.0, in1=rest2[:], op0=ALU.mult, op1=ALU.add
+            )
 
         w_grouped = {}
         w_codes = {}
         w_scales = {}
 
-        def regroup_weight(t):
-            if not 0 <= t < KINDS:
-                return
-            grouped = stage.tile([P, D, PACK], BF16, align_bytes=64, name="w_grouped")
+        def regroup_weight(t, half):
+            if half == 0:
+                w_grouped[t] = stage.tile([P, D, PACK], BF16, align_bytes=64, name="w_grouped")
+            cols = slice(D // 2 * half, D // 2 * half + D // 2)
             nc.scalar.copy(
-                out=grouped[:].rearrange("p (c i) t -> p c t i", i=4),
-                in_=w_raw[t][:].rearrange("p t (c i) -> p c t i", i=4),
+                out=w_grouped[t][:, cols, :].rearrange("p (c i) t -> p c t i", i=4),
+                in_=w_raw[t][:, :, cols].rearrange("p t (c i) -> p c t i", i=4),
             )
-            w_grouped[t] = grouped
 
         def quantise_weight(t):
-            if not 0 <= t < KINDS:
-                return
             w_codes[t] = keep.tile([P, D], U32, align_bytes=64, name="w_codes%d" % t)
             w_scales[t] = keep.tile([P, D], U8, align_bytes=64, name="w_scales%d" % t)
             nc.vector.quantize_mx(
@@ -145,164 +154,255 @@ def tile_dcadecoderblock_pa_t_kernel(
         x_codes = {}
         x_scales = {}
 
-        def transpose_x(index):
-            if not 0 <= index < STEPS:
+        def transpose_x(q):
+            if q >= PHASES:
                 return
-            g, i, l = split(index)
+            g, l, i = split_tile(2 * q)
             words = x_sb[(g, l)][:].bitcast(F32)
-            xt = psum.tile([P, 2, P], F32, tag="xt", name="xt")
-            for u in range(2):
-                nc.tensor.transpose(xt[:, u, :], words[:, i, u : 2 * P : 2], ident_f[:])
-            grouped = stage.tile([P, P, PACK], BF16, align_bytes=64, bufs=3, name="x_grouped")
-            nc.scalar.copy(out=grouped[:].bitcast(F32), in_=xt[:].rearrange("p u r -> p r u"))
-            x_grouped[index] = grouped
+            if g == 0:
+                xt = psum.tile([P, 2, 2, P], F32, tag="back", bufs=2, name="xt")
+            else:
+                xt = psum.tile([P, 2, 2, P], F32, tag="xt", name="xt")
+            for n in range(2):
+                for u in range(2):
+                    nc.tensor.transpose(xt[:, n, u, :], words[:, i + n, u : 2 * P : 2], ident_f[:])
+            x_grouped[q] = stage.tile([P, 2, P, PACK], BF16, align_bytes=64, bufs=3, name="x_grouped")
+            nc.scalar.copy(
+                out=x_grouped[q][:].rearrange("p n r t -> p (n r t)").bitcast(F32).rearrange("p (n r u) -> p n r u", n=2, u=2),
+                in_=xt[:].rearrange("p n u r -> p n r u"),
+            )
 
-        def quantise_x(index):
-            if not 0 <= index < STEPS:
+        def quantise_x(q):
+            if q >= PHASES:
                 return
-            g, i, l = split(index)
+            g, l, i = split_tile(2 * q)
             if i == 0:
                 x_codes[(g, l)] = stage.tile([P, TILES * P], U32, align_bytes=64, bufs=6, name="x_codes")
                 x_scales[(g, l)] = stage.tile([P, TILES * P], U8, align_bytes=64, bufs=6, name="x_scales")
             nc.vector.quantize_mx(
-                out=x_codes[(g, l)][:, P * i : P * i + P].bitcast(FP8X4),
-                scales=x_scales[(g, l)][:, P * i : P * i + P],
-                in_=x_grouped[index][:].rearrange("p r t -> p (r t)"),
+                out=x_codes[(g, l)][:, P * i : P * i + 2 * P].bitcast(FP8X4),
+                scales=x_scales[(g, l)][:, P * i : P * i + 2 * P],
+                in_=x_grouped[q][:].rearrange("p n r t -> p (n r t)"),
             )
 
         stats = {}
-        mean_var = {}
+        normed = {}
+        total = {}
+        neg_mean = {}
         std = {}
         rstd = {}
         offset = {}
-        normed = {}
 
-        def statistics(index):
-            if not 0 <= index < STEPS:
+        def statistics(s):
+            if s >= ROW_TILES:
                 return
-            g, i, l = split(index)
-            if l == 0:
-                stats[(g, i)] = small.tile([P, LAYERS, 6], F32, name="stats")
-            nc.vector.bn_stats(out=stats[(g, i)][:, l, :], in_=x_sb[(g, l)][:, i, :])
+            g, l, i = split_tile(s)
+            if i == 0:
+                stats[(g, l)] = small.tile([P, TILES, 6], F32, name="stats")
+            nc.vector.bn_stats(out=stats[(g, l)][:, i, :], in_=x_sb[(g, l)][:, i, :])
 
-        def aggregate(index):
-            if not 0 <= index < STEPS:
+        def moments(s, engine):
+            if s >= ROW_TILES or s % TILES != TILES - 1:
                 return
-            g, i, l = split(index)
-            if l == 0:
-                mean_var[(g, i)] = small.tile([P, LAYERS, 2], F32, name="mean_var")
-            nc.vector.bn_aggr(out=mean_var[(g, i)][:, l, :], in_=stats[(g, i)][:, l, :])
+            g, l, i = split_tile(s)
+            st = stats[(g, l)]
+            diff = small.tile([P, TILES], F32, name="diff")
+            half = small.tile([P, TILES], F32, name="half")
+            both = small.tile([P, TILES], F32, name="both")
+            mean2 = small.tile([P, TILES], F32, name="mean2")
+            total[(g, l)] = small.tile([P, TILES], F32, name="tot")
+            neg_mean[(g, l)] = small.tile([P, TILES], F32, name="neg")
+            engine.tensor_tensor(out=diff[:], in0=st[:, :, 1], in1=st[:, :, 4], op=ALU.subtract)
+            engine.tensor_tensor(out=both[:], in0=st[:, :, 2], in1=st[:, :, 5], op=ALU.add)
+            engine.tensor_scalar(
+                out=half[:], in0=diff[:], scalar1=float(D // 4), scalar2=0.0, op0=ALU.mult, op1=ALU.add
+            )
+            engine.tensor_tensor(out=mean2[:], in0=st[:, :, 1], in1=st[:, :, 4], op=ALU.add)
+            engine.tensor_tensor(out=half[:], in0=half[:], in1=diff[:], op=ALU.mult)
+            engine.tensor_scalar(
+                out=neg_mean[(g, l)][:], in0=mean2[:], scalar1=-0.5, scalar2=0.0, op0=ALU.mult, op1=ALU.add
+            )
+            engine.tensor_tensor(out=total[(g, l)][:], in0=half[:], in1=both[:], op=ALU.add)
 
-        def deviation(index):
-            if not 0 <= index < STEPS:
+        def deviation(s):
+            if s >= ROW_TILES or s % TILES:
                 return
-            g, i, l = split(index)
-            if l == LAYERS - 1:
-                std[(g, i)] = small.tile([P, LAYERS], F32, name="std")
-                nc.scalar.activation(
-                    out=std[(g, i)][:], in_=mean_var[(g, i)][:, :, 1], func=ACT.Sqrt, bias=eps[:], scale=1.0
-                )
+            g, l, i = split_tile(s)
+            std[(g, l)] = small.tile([P, TILES], F32, name="std")
+            nc.scalar.activation(out=std[(g, l)][:], in_=total[(g, l)][:], func=ACT.Sqrt, bias=eps[:], scale=1.0 / D)
 
-        def reciprocal(index):
-            if not 0 <= index < STEPS:
+        def reciprocal(s):
+            if s >= ROW_TILES or s % TILES:
                 return
-            g, i, l = split(index)
-            if l == LAYERS - 1:
-                rstd[(g, i)] = small.tile([P, LAYERS], F32, name="rstd")
-                nc.vector.reciprocal(out=rstd[(g, i)][:], in_=std[(g, i)][:])
-                offset[(g, i)] = small.tile([P, LAYERS], F32, name="offset")
-                nc.vector.scalar_tensor_tensor(
-                    out=offset[(g, i)][:], in0=mean_var[(g, i)][:, :, 0], scalar=-1.0, in1=rstd[(g, i)][:],
-                    op0=ALU.mult, op1=ALU.mult,
-                )
+            g, l, i = split_tile(s)
+            rstd[(g, l)] = small.tile([P, TILES], F32, name="rstd")
+            nc.vector.reciprocal(out=rstd[(g, l)][:], in_=std[(g, l)][:])
+            offset[(g, l)] = small.tile([P, TILES], F32, name="offset")
+            nc.gpsimd.tensor_tensor(
+                out=offset[(g, l)][:], in0=neg_mean[(g, l)][:], in1=rstd[(g, l)][:], op=ALU.mult
+            )
 
-        def scale(index):
-            if not 0 <= index < STEPS:
+        def scale(s):
+            if s >= ROW_TILES:
                 return
-            g, i, l = split(index)
-            y = stage.tile([P, D], F32, bufs=2 * PER_GROUP, name="normed")
+            g, l, i = split_tile(s)
+            y = stage.tile([P, D], F32, bufs=2 * LAYERS * TILES, name="normed")
             nc.gpsimd.tensor_scalar(
                 out=y[:], in0=x_sb[(g, l)][:, i, :],
-                scalar1=rstd[(g, i)][:, l : l + 1], scalar2=offset[(g, i)][:, l : l + 1],
+                scalar1=rstd[(g, l)][:, i : i + 1], scalar2=offset[(g, l)][:, i : i + 1],
                 op0=ALU.mult, op1=ALU.add,
             )
-            normed[(g, i, l)] = y
+            normed[(g, l, i)] = y
 
         nt = {}
         acc = {}
 
-        def transpose_normed(index):
-            if not 0 <= index < STEPS:
-                return
-            g, j, third = split(index)
-            if third == 0:
-                nt[(g, j)] = psum.tile([P, TILES * P], F32, tag="nt", bufs=2, name="nt")
-            for n in range(TILES * third, TILES * third + TILES):
-                i, l = divmod(n, LAYERS)
-                nc.tensor.matmul(
-                    out=nt[(g, j)][:, P * i : P * i + P],
-                    lhsT=normed[(g, i, l)][:, P * j : P * j + P],
-                    rhs=ident_f[:],
-                    is_transpose=True,
-                    start=(l == 0),
-                    stop=(l == LAYERS - 1),
-                )
+        def blocks_of_phase(p):
+            return [u // KINDS for u in (2 * p, 2 * p + 1) if u % KINDS == 0 and 0 <= u < UNITS]
 
-        def seed(index):
-            if not 0 <= index < STEPS:
-                return
-            g, j, t = split(index)
-            a = stage.tile([P, TILES * P], F32, bufs=10, name="acc")
-            nc.scalar.activation(
-                out=a[:], in_=nt[(g, j)][:], func=ACT.Identity,
-                scale=gain[:, t, j : j + 1], bias=rest[:, t, j : j + 1],
-            )
-            acc[(g, t, j)] = a
+        def fill_nt(p):
+            for b in blocks_of_phase(p):
+                g, j = divmod(b, BLOCKS)
+                nt[b] = psum.tile([P, TILES * P], F32, tag="nt", name="nt")
+                for i in range(TILES):
+                    for l in range(LAYERS):
+                        nc.tensor.matmul(
+                            out=nt[b][:, P * i : P * i + P],
+                            lhsT=normed[(g, l, i)][:, P * j : P * j + P],
+                            rhs=ident_f[:],
+                            is_transpose=True,
+                            start=(l == 0),
+                            stop=(l == LAYERS - 1),
+                        )
 
-        def products(index):
-            if not 0 <= index < STEPS:
-                return
-            g, j, l = split(index)
+        def seed(p):
+            for b in blocks_of_phase(p):
+                j = b % BLOCKS
+                for t in range(KINDS):
+                    u = KINDS * b + t
+                    rest = rest2 if on_scalar(u) else rest3
+                    acc[u] = stage.tile([P, TILES * P], F32, bufs=12, name="acc")
+                    nc.scalar.activation(
+                        out=acc[u][:], in_=nt[b][:], func=ACT.Identity,
+                        scale=gain[:, t, j : j + 1], bias=rest[:, t, j : j + 1],
+                    )
+
+        relued = {}
+
+        def product(u, l):
+            g, j, t = split_unit(u)
             cols = slice(P * j, P * j + P)
-            for t in range(KINDS):
-                prod = psum.tile([P, TILES * P], F32, tag="prod", bufs=3, name="prod")
-                nc.tensor.matmul_mx(
-                    out=prod[:],
-                    lhsT=w_codes[t][:, cols].bitcast(FP8X4),
-                    lhsT_scale=w_scales[t][:, cols],
-                    rhs=x_codes[(g, l)][:].bitcast(FP8X4),
-                    rhs_scale=x_scales[(g, l)][:],
-                    start=True,
-                    stop=True,
+            prod = psum.tile([P, TILES * P], F32, tag="prod", bufs=4, name="prod")
+            nc.tensor.matmul_mx(
+                out=prod[:],
+                lhsT=w_codes[t][:, cols].bitcast(FP8X4),
+                lhsT_scale=w_scales[t][:, cols],
+                rhs=x_codes[(g, l)][:].bitcast(FP8X4),
+                rhs_scale=x_scales[(g, l)][:],
+                start=True,
+                stop=True,
+            )
+            if l == LAYERS - 1 and on_scalar(u):
+                relued[u] = stage.tile([P, TILES * P], F32, bufs=4, name="relued")
+                nc.scalar.activation(
+                    out=relued[u][:], in_=prod[:], func=ACT.Relu, bias=bias[:, t, j : j + 1], scale=1.0
                 )
+            else:
                 nc.vector.scalar_tensor_tensor(
-                    out=acc[(g, t, j)][:], in0=prod[:], scalar=neg_bias[:, t, j : j + 1],
-                    in1=acc[(g, t, j)][:], op0=ALU.max, op1=ALU.add,
+                    out=acc[u][:], in0=prod[:], scalar=neg_bias[:, t, j : j + 1],
+                    in1=acc[u][:], op0=ALU.max, op1=ALU.add,
                 )
 
-        def back(index):
-            if not 0 <= index < STEPS:
+        def back(u):
+            if not 0 <= u < UNITS:
                 return
-            g, j, t = split(index)
+            g, j, t = split_unit(u)
+            parts = [acc[u], relued[u]] if on_scalar(u) else [acc[u]]
             turned = psum.tile([P, TILES, P], F32, tag="back", bufs=2, name="turned")
             for i in range(TILES):
-                nc.tensor.transpose(turned[:, i, :], acc[(g, t, j)][:, P * i : P * i + P], ident_f[:])
+                for n, part in enumerate(parts):
+                    nc.tensor.matmul(
+                        out=turned[:, i, :],
+                        lhsT=part[:, P * i : P * i + P],
+                        rhs=ident_f[:],
+                        is_transpose=True,
+                        start=(n == 0),
+                        stop=(n == len(parts) - 1),
+                    )
             result = stage.tile([P, TILES, P], F32, bufs=4, name="result")
             nc.scalar.copy(out=result[:], in_=turned[:])
             nc.sync.dma_start(out=rows_of_group(outs[t], g)[:, :, P * j : P * j + P], in_=result[:])
 
-        for step in range(-LEAD_STATS, STEPS + LAG_BACK):
-            products(step)
-            deviation(step + LEAD_STD)
-            seed(step + LEAD_SEED)
-            back(step - LAG_BACK)
-            transpose_normed(step + LEAD_NT)
-            transpose_x(step + LEAD_XT)
-            regroup_weight(step + LEAD_WEIGHTS)
-            constants(step + LEAD_CONSTANTS)
-            statistics(step + LEAD_STATS)
-            quantise_x(step + LEAD_QUANTISE)
-            quantise_weight(step + LEAD_WEIGHTS - 1)
-            aggregate(step + LEAD_STATS)
-            reciprocal(step + LEAD_RSTD)
-            scale(step + LEAD_SCALE)
+        warm = small.tile([P, 1], F32, name="warm")
+        nc.scalar.activation(out=warm[:], in_=eps[:], func=ACT.Sqrt, bias=eps[:], scale=1.0)
+
+        def layer_statistics(l):
+            for i in range(TILES):
+                statistics(TILES * l + i)
+            moments(TILES * l + TILES - 1, nc.vector)
+
+        def layer_scale(l):
+            deviation(TILES * l)
+            reciprocal(TILES * l)
+            for i in range(TILES):
+                scale(TILES * l + i)
+
+        layer_statistics(0)
+        transpose_x(0)
+        transpose_x(1)
+        quantise_x(0)
+        quantise_x(1)
+        regroup_weight(0, 0)
+        layer_scale(0)
+        regroup_weight(0, 1)
+        layer_statistics(1)
+        transpose_x(2)
+        transpose_x(3)
+        quantise_x(2)
+        quantise_x(3)
+        regroup_weight(1, 0)
+        layer_scale(1)
+        regroup_weight(1, 1)
+        layer_statistics(2)
+        transpose_x(4)
+        transpose_x(5)
+        quantise_weight(0)
+        quantise_x(4)
+        quantise_x(5)
+        layer_scale(2)
+        constants()
+        quantise_weight(1)
+        regroup_weight(2, 0)
+        regroup_weight(2, 1)
+
+        for p in range(-LEAD_FILL - 1, PHASES + 1):
+            live = 0 <= p < PHASES
+            a, b = 2 * p, 2 * p + 1
+            if live:
+                product(a, 0)
+                product(b, 0)
+                product(a, 2)
+                product(a, 1)
+                product(b, 1)
+            if p + LEAD_STATS >= PHASES // GROUPS:
+                statistics(2 * (p + LEAD_STATS))
+            if live:
+                product(b, 2)
+            seed(p + LEAD_FILL - 1)
+            back(a - 2)
+            back(b - 2)
+            if p + LEAD_QUANTISE >= PHASES // GROUPS:
+                quantise_x(p + LEAD_QUANTISE)
+            if p == -1:
+                quantise_weight(2)
+            if p + LEAD_SCALE >= PHASES // GROUPS:
+                deviation(2 * (p + LEAD_SCALE))
+                reciprocal(2 * (p + LEAD_SCALE))
+                scale(2 * (p + LEAD_SCALE))
+                scale(2 * (p + LEAD_SCALE) + 1)
+            if p + LEAD_STATS >= PHASES // GROUPS:
+                statistics(2 * (p + LEAD_STATS) + 1)
+                moments(2 * (p + LEAD_STATS) + 1, nc.gpsimd)
+            if p + LEAD_XT >= PHASES // GROUPS:
+                transpose_x(p + LEAD_XT)
+            fill_nt(p + LEAD_FILL)

@@ -21,15 +21,17 @@ GROUPS = BATCH * HALVES
 BLOCKS = D // P
 KINDS = 3
 
-UNITS = GROUPS * BLOCKS * KINDS
-PHASES = UNITS // 2
-ROW_TILES = GROUPS * LAYERS * TILES
+STEPS = GROUPS * BLOCKS * KINDS
+PER_GROUP = BLOCKS * KINDS
+PAIRS = STEPS // 2
 
-LEAD_FILL = 2
-LEAD_XT = 7
-LEAD_QUANTISE = 6
-LEAD_SCALE = 7
-LEAD_STATS = 9
+LEAD_SEED = 1
+LEAD_FILL = 4
+LEAD_XT = 13
+LEAD_QUANTISE = 11
+LEAD_SCALE = 13
+LEAD_STATS = 17
+LAG_BACK = 2
 
 FLOPS = 2 * BATCH * LAYERS * SEQ * D * KINDS * D
 
@@ -155,7 +157,7 @@ def tile_dcadecoderblock_pa_t_kernel(
         x_scales = {}
 
         def transpose_x(q):
-            if q >= PHASES:
+            if q >= PAIRS:
                 return
             g, l, i = split_tile(2 * q)
             words = x_sb[(g, l)][:].bitcast(F32)
@@ -173,7 +175,7 @@ def tile_dcadecoderblock_pa_t_kernel(
             )
 
         def quantise_x(q):
-            if q >= PHASES:
+            if q >= PAIRS:
                 return
             g, l, i = split_tile(2 * q)
             if i == 0:
@@ -194,7 +196,7 @@ def tile_dcadecoderblock_pa_t_kernel(
         offset = {}
 
         def statistics(s):
-            if s >= ROW_TILES:
+            if s >= STEPS:
                 return
             g, l, i = split_tile(s)
             if i == 0:
@@ -202,7 +204,7 @@ def tile_dcadecoderblock_pa_t_kernel(
             nc.vector.bn_stats(out=stats[(g, l)][:, i, :], in_=x_sb[(g, l)][:, i, :])
 
         def moments(s, engine):
-            if s >= ROW_TILES or s % TILES != TILES - 1:
+            if s >= STEPS or s % TILES != TILES - 1:
                 return
             g, l, i = split_tile(s)
             st = stats[(g, l)]
@@ -225,14 +227,14 @@ def tile_dcadecoderblock_pa_t_kernel(
             engine.tensor_tensor(out=total[(g, l)][:], in0=half[:], in1=both[:], op=ALU.add)
 
         def deviation(s):
-            if s >= ROW_TILES or s % TILES:
+            if s >= STEPS or s % TILES:
                 return
             g, l, i = split_tile(s)
             std[(g, l)] = small.tile([P, TILES], F32, name="std")
             nc.scalar.activation(out=std[(g, l)][:], in_=total[(g, l)][:], func=ACT.Sqrt, bias=eps[:], scale=1.0 / D)
 
         def reciprocal(s):
-            if s >= ROW_TILES or s % TILES:
+            if s >= STEPS or s % TILES:
                 return
             g, l, i = split_tile(s)
             rstd[(g, l)] = small.tile([P, TILES], F32, name="rstd")
@@ -243,7 +245,7 @@ def tile_dcadecoderblock_pa_t_kernel(
             )
 
         def scale(s):
-            if s >= ROW_TILES:
+            if s >= STEPS:
                 return
             g, l, i = split_tile(s)
             y = stage.tile([P, D], F32, bufs=2 * LAYERS * TILES, name="normed")
@@ -257,42 +259,40 @@ def tile_dcadecoderblock_pa_t_kernel(
         nt = {}
         acc = {}
 
-        def blocks_of_phase(p):
-            return [u // KINDS for u in (2 * p, 2 * p + 1) if u % KINDS == 0 and 0 <= u < UNITS]
+        def fill_nt(u):
+            if not 0 <= u < STEPS:
+                return
+            g, j, third = split_unit(u)
+            if third == 0:
+                nt[(g, j)] = psum.tile([P, TILES * P], F32, tag="nt", bufs=2, name="nt")
+            for n in range(TILES * third, TILES * third + TILES):
+                i, l = divmod(n, LAYERS)
+                nc.tensor.matmul(
+                    out=nt[(g, j)][:, P * i : P * i + P],
+                    lhsT=normed[(g, l, i)][:, P * j : P * j + P],
+                    rhs=ident_f[:],
+                    is_transpose=True,
+                    start=(l == 0),
+                    stop=(l == LAYERS - 1),
+                )
 
-        def fill_nt(p):
-            for b in blocks_of_phase(p):
-                g, j = divmod(b, BLOCKS)
-                nt[b] = psum.tile([P, TILES * P], F32, tag="nt", name="nt")
-                for i in range(TILES):
-                    for l in range(LAYERS):
-                        nc.tensor.matmul(
-                            out=nt[b][:, P * i : P * i + P],
-                            lhsT=normed[(g, l, i)][:, P * j : P * j + P],
-                            rhs=ident_f[:],
-                            is_transpose=True,
-                            start=(l == 0),
-                            stop=(l == LAYERS - 1),
-                        )
-
-        def seed(p):
-            for b in blocks_of_phase(p):
-                j = b % BLOCKS
-                for t in range(KINDS):
-                    u = KINDS * b + t
-                    rest = rest2 if on_scalar(u) else rest3
-                    acc[u] = stage.tile([P, TILES * P], F32, bufs=12, name="acc")
-                    nc.scalar.activation(
-                        out=acc[u][:], in_=nt[b][:], func=ACT.Identity,
-                        scale=gain[:, t, j : j + 1], bias=rest[:, t, j : j + 1],
-                    )
+        def seed(u):
+            if not 0 <= u < STEPS:
+                return
+            g, j, t = split_unit(u)
+            rest = rest2 if on_scalar(u) else rest3
+            acc[u] = stage.tile([P, TILES * P], F32, bufs=6, name="acc")
+            nc.scalar.activation(
+                out=acc[u][:], in_=nt[(g, j)][:], func=ACT.Identity,
+                scale=gain[:, t, j : j + 1], bias=rest[:, t, j : j + 1],
+            )
 
         relued = {}
 
         def product(u, l):
             g, j, t = split_unit(u)
             cols = slice(P * j, P * j + P)
-            prod = psum.tile([P, TILES * P], F32, tag="prod", bufs=4, name="prod")
+            prod = psum.tile([P, TILES * P], F32, tag="prod", bufs=3, name="prod")
             nc.tensor.matmul_mx(
                 out=prod[:],
                 lhsT=w_codes[t][:, cols].bitcast(FP8X4),
@@ -314,7 +314,7 @@ def tile_dcadecoderblock_pa_t_kernel(
                 )
 
         def back(u):
-            if not 0 <= u < UNITS:
+            if not 0 <= u < STEPS:
                 return
             g, j, t = split_unit(u)
             parts = [acc[u], relued[u]] if on_scalar(u) else [acc[u]]
@@ -375,34 +375,38 @@ def tile_dcadecoderblock_pa_t_kernel(
         regroup_weight(2, 0)
         regroup_weight(2, 1)
 
-        for p in range(-LEAD_FILL - 1, PHASES + 1):
-            live = 0 <= p < PHASES
-            a, b = 2 * p, 2 * p + 1
+        def after_first(index, work, *arguments):
+            if index >= PER_GROUP:
+                work(*arguments)
+
+        for u in range(PER_GROUP - LEAD_STATS, STEPS + LAG_BACK):
+            live = 0 <= u < STEPS
+            odd = u % 2 == 1
             if live:
-                product(a, 0)
-                product(b, 0)
-                product(a, 2)
-                product(a, 1)
-                product(b, 1)
-            if p + LEAD_STATS >= PHASES // GROUPS:
-                statistics(2 * (p + LEAD_STATS))
+                product(u, 0)
+            if odd:
+                after_first(u + LEAD_QUANTISE, quantise_x, (u + LEAD_QUANTISE) // 2)
+            else:
+                after_first(u + LEAD_STATS, statistics, u + LEAD_STATS)
+            if live and on_scalar(u):
+                product(u, 2)
             if live:
-                product(b, 2)
-            seed(p + LEAD_FILL - 1)
-            back(a - 2)
-            back(b - 2)
-            if p + LEAD_QUANTISE >= PHASES // GROUPS:
-                quantise_x(p + LEAD_QUANTISE)
-            if p == -1:
+                product(u, 1)
+            if odd:
+                after_first(u + LEAD_STATS, statistics, u + LEAD_STATS)
+            if live and not on_scalar(u):
+                product(u, 2)
+            back(u - LAG_BACK)
+            fill_nt(u + LEAD_FILL)
+            seed(u + LEAD_SEED)
+            if odd:
+                after_first(u + LEAD_XT, transpose_x, (u + LEAD_XT) // 2)
+            if u == -1:
                 quantise_weight(2)
-            if p + LEAD_SCALE >= PHASES // GROUPS:
-                deviation(2 * (p + LEAD_SCALE))
-                reciprocal(2 * (p + LEAD_SCALE))
-                scale(2 * (p + LEAD_SCALE))
-                scale(2 * (p + LEAD_SCALE) + 1)
-            if p + LEAD_STATS >= PHASES // GROUPS:
-                statistics(2 * (p + LEAD_STATS) + 1)
-                moments(2 * (p + LEAD_STATS) + 1, nc.gpsimd)
-            if p + LEAD_XT >= PHASES // GROUPS:
-                transpose_x(p + LEAD_XT)
-            fill_nt(p + LEAD_FILL)
+            after_first(u + LEAD_SCALE, deviation, u + LEAD_SCALE)
+            after_first(u + LEAD_SCALE, reciprocal, u + LEAD_SCALE)
+            m, within = divmod(u + LEAD_SCALE, TILES)
+            if within < 2:
+                after_first(TILES * m, scale, TILES * m + 2 * within)
+                after_first(TILES * m, scale, TILES * m + 2 * within + 1)
+            after_first(u + LEAD_STATS, moments, u + LEAD_STATS, nc.gpsimd)

@@ -25,13 +25,20 @@ STEPS = GROUPS * BLOCKS * KINDS
 PER_GROUP = BLOCKS * KINDS
 PAIRS = STEPS // 2
 
-LEAD_SEED = 1
-LEAD_FILL = 4
-LEAD_XT = 13
-LEAD_QUANTISE = 11
-LEAD_SCALE = 13
-LEAD_STATS = 17
-LAG_BACK = 2
+LEAD_SEED = 3
+LEAD_FILL = 6
+LEAD_XT = 14
+LEAD_QUANTISE = 12
+LEAD_SCALE = 15
+LEAD_STATS = 19
+LAG_BACK = 3
+ON_S = ((0,0,0),(0,2,2),(1,1,1))
+RB = 6
+ORD = (0.5,)
+S_TILES = ()
+YS = 0
+NP, NN, NB = 3, 2, 2
+VORD = 'a'
 
 FLOPS = 2 * BATCH * LAYERS * SEQ * D * KINDS * D
 
@@ -91,8 +98,8 @@ def tile_dcadecoderblock_pa_t_kernel(
         make_identity(nc, ident_f[:])
         ident_b = keep.tile([P, P], BF16, name="ident_b")
         make_identity(nc, ident_b[:])
-        eps = keep.tile([P, 1], F32, name="eps")
-        nc.vector.memset(eps[:], EPS)
+        power = keep.tile([P, TILES], F32, name="power")
+        nc.vector.memset(power[:], -0.5)
 
         vec_cols = keep.tile([P, KINDS, 3, BLOCKS], F32, name="vec_cols")
         bias = vec_cols[:, :, 0, :]
@@ -112,8 +119,11 @@ def tile_dcadecoderblock_pa_t_kernel(
             l, i = divmod(within, TILES)
             return g, l, i
 
-        def on_scalar(u):
-            return u % 2 == 0
+        def on_scalar(u, l):
+            return (u // 3 % 2, u % 3, l) in ON_S
+
+        def scalar_layers(u):
+            return [l for l in range(LAYERS) if on_scalar(u, l)]
 
         def constants():
             vec_ps = psum.tile([P, P], BF16, tag="xt", name="vec_ps")
@@ -162,13 +172,13 @@ def tile_dcadecoderblock_pa_t_kernel(
             g, l, i = split_tile(2 * q)
             words = x_sb[(g, l)][:].bitcast(F32)
             if g == 0:
-                xt = psum.tile([P, 2, 2, P], F32, tag="back", bufs=2, name="xt")
+                xt = psum.tile([P, 2, 2, P], F32, tag="back", bufs=NB, name="xt")
             else:
                 xt = psum.tile([P, 2, 2, P], F32, tag="xt", name="xt")
             for n in range(2):
                 for u in range(2):
                     nc.tensor.transpose(xt[:, n, u, :], words[:, i + n, u : 2 * P : 2], ident_f[:])
-            x_grouped[q] = stage.tile([P, 2, P, PACK], BF16, align_bytes=64, bufs=3, name="x_grouped")
+            x_grouped[q] = stage.tile([P, 2, P, PACK], BF16, align_bytes=64, bufs=4, name="x_grouped")
             nc.scalar.copy(
                 out=x_grouped[q][:].rearrange("p n r t -> p (n r t)").bitcast(F32).rearrange("p (n r u) -> p n r u", n=2, u=2),
                 in_=xt[:].rearrange("p n u r -> p n r u"),
@@ -191,7 +201,6 @@ def tile_dcadecoderblock_pa_t_kernel(
         normed = {}
         total = {}
         neg_mean = {}
-        std = {}
         rstd = {}
         offset = {}
 
@@ -201,9 +210,32 @@ def tile_dcadecoderblock_pa_t_kernel(
             g, l, i = split_tile(s)
             if i == 0:
                 stats[(g, l)] = small.tile([P, TILES, 6], F32, name="stats")
-            nc.vector.bn_stats(out=stats[(g, l)][:, i, :], in_=x_sb[(g, l)][:, i, :])
+            if g > 0 and i in S_TILES:
+                s_first(g, l, i)
+            else:
+                nc.vector.bn_stats(out=stats[(g, l)][:, i, :], in_=x_sb[(g, l)][:, i, :])
 
-        def moments(s, engine):
+        s_sum = {}
+        s_tot = {}
+        s_neg = {}
+
+        def s_first(g, l, i):
+            junk = stage.tile([P, D], BF16, name="junk")
+            s_sum[(g, l, i)] = small.tile([P, 1], F32, name="s_sum")
+            nc.scalar.activation(out=junk[:], in_=x_sb[(g, l)][:, i, :], func=ACT.Identity, accum_out=s_sum[(g, l, i)][:])
+            s_neg[(g, l, i)] = small.tile([P, 1], F32, name="s_neg")
+            nc.gpsimd.tensor_scalar(out=s_neg[(g, l, i)][:], in0=s_sum[(g, l, i)][:], scalar1=-1.0 / D, scalar2=0.0, op0=ALU.mult, op1=ALU.add)
+
+        def s_second(s):
+            if not 0 <= s < STEPS:
+                return
+            g, l, i = split_tile(s)
+            if g > 0 and i in S_TILES:
+                junk = stage.tile([P, D], BF16, name="junk")
+                s_tot[(g, l, i)] = small.tile([P, 1], F32, name="s_tot")
+                nc.scalar.activation(out=junk[:], in_=x_sb[(g, l)][:, i, :], func=ACT.Square, bias=s_neg[(g, l, i)][:], accum_out=s_tot[(g, l, i)][:])
+
+        def moments(s):
             if s >= STEPS or s % TILES != TILES - 1:
                 return
             g, l, i = split_tile(s)
@@ -211,38 +243,26 @@ def tile_dcadecoderblock_pa_t_kernel(
             diff = small.tile([P, TILES], F32, name="diff")
             half = small.tile([P, TILES], F32, name="half")
             both = small.tile([P, TILES], F32, name="both")
+            var = small.tile([P, TILES], F32, name="var")
             mean2 = small.tile([P, TILES], F32, name="mean2")
-            total[(g, l)] = small.tile([P, TILES], F32, name="tot")
-            neg_mean[(g, l)] = small.tile([P, TILES], F32, name="neg")
-            engine.tensor_tensor(out=diff[:], in0=st[:, :, 1], in1=st[:, :, 4], op=ALU.subtract)
-            engine.tensor_tensor(out=both[:], in0=st[:, :, 2], in1=st[:, :, 5], op=ALU.add)
-            engine.tensor_scalar(
+            neg_mean = small.tile([P, TILES], F32, name="neg_mean")
+            rstd[(g, l)] = small.tile([P, TILES], F32, name="rstd")
+            offset[(g, l)] = small.tile([P, TILES], F32, name="offset")
+            pool = nc.gpsimd
+            pool.tensor_tensor(out=diff[:], in0=st[:, :, 1], in1=st[:, :, 4], op=ALU.subtract)
+            pool.tensor_tensor(out=both[:], in0=st[:, :, 2], in1=st[:, :, 5], op=ALU.add)
+            pool.tensor_scalar(
                 out=half[:], in0=diff[:], scalar1=float(D // 4), scalar2=0.0, op0=ALU.mult, op1=ALU.add
             )
-            engine.tensor_tensor(out=mean2[:], in0=st[:, :, 1], in1=st[:, :, 4], op=ALU.add)
-            engine.tensor_tensor(out=half[:], in0=half[:], in1=diff[:], op=ALU.mult)
-            engine.tensor_scalar(
-                out=neg_mean[(g, l)][:], in0=mean2[:], scalar1=-0.5, scalar2=0.0, op0=ALU.mult, op1=ALU.add
+            pool.tensor_tensor(out=half[:], in0=half[:], in1=diff[:], op=ALU.mult)
+            pool.tensor_tensor(out=var[:], in0=half[:], in1=both[:], op=ALU.add)
+            pool.tensor_scalar(out=var[:], in0=var[:], scalar1=1.0 / D, scalar2=EPS, op0=ALU.mult, op1=ALU.add)
+            pool.tensor_tensor(out=rstd[(g, l)][:], in0=var[:], in1=power[:], op=ALU.pow)
+            pool.tensor_tensor(out=mean2[:], in0=st[:, :, 1], in1=st[:, :, 4], op=ALU.add)
+            pool.tensor_scalar(
+                out=neg_mean[:], in0=mean2[:], scalar1=-0.5, scalar2=0.0, op0=ALU.mult, op1=ALU.add
             )
-            engine.tensor_tensor(out=total[(g, l)][:], in0=half[:], in1=both[:], op=ALU.add)
-
-        def deviation(s):
-            if s >= STEPS or s % TILES:
-                return
-            g, l, i = split_tile(s)
-            std[(g, l)] = small.tile([P, TILES], F32, name="std")
-            nc.scalar.activation(out=std[(g, l)][:], in_=total[(g, l)][:], func=ACT.Sqrt, bias=eps[:], scale=1.0 / D)
-
-        def reciprocal(s):
-            if s >= STEPS or s % TILES:
-                return
-            g, l, i = split_tile(s)
-            rstd[(g, l)] = small.tile([P, TILES], F32, name="rstd")
-            nc.vector.reciprocal(out=rstd[(g, l)][:], in_=std[(g, l)][:])
-            offset[(g, l)] = small.tile([P, TILES], F32, name="offset")
-            nc.gpsimd.tensor_tensor(
-                out=offset[(g, l)][:], in0=neg_mean[(g, l)][:], in1=rstd[(g, l)][:], op=ALU.mult
-            )
+            pool.tensor_tensor(out=offset[(g, l)][:], in0=neg_mean[:], in1=rstd[(g, l)][:], op=ALU.mult)
 
         def scale(s):
             if s >= STEPS:
@@ -255,6 +275,8 @@ def tile_dcadecoderblock_pa_t_kernel(
                 op0=ALU.mult, op1=ALU.add,
             )
             normed[(g, l, i)] = y
+            if g > 0 and 0 < l <= YS:
+                nc.gpsimd.tensor_tensor(out=normed[(g, 0, i)][:], in0=normed[(g, 0, i)][:], in1=y[:], op=ALU.add)
 
         nt = {}
         acc = {}
@@ -264,24 +286,38 @@ def tile_dcadecoderblock_pa_t_kernel(
                 return
             g, j, third = split_unit(u)
             if third == 0:
-                nt[(g, j)] = psum.tile([P, TILES * P], F32, tag="nt", bufs=2, name="nt")
-            for n in range(TILES * third, TILES * third + TILES):
-                i, l = divmod(n, LAYERS)
+                nt[(g, j)] = psum.tile([P, TILES * P], F32, tag="nt", bufs=NN, name="nt")
+            layers = [0] + [l for l in (1, 2) if l > YS or g == 0]
+            k = len(layers)
+            todo = range(TILES * k)
+            if NN == 1:
+                if third:
+                    return
+            elif YS == 2 and g > 0:
+                if third:
+                    return
+            elif YS == 1 and g > 0:
+                todo = [range(0, 4), range(4, 8), ()][third] if NN > 1 else ([range(8), (), ()][third])
+            else:
+                todo = range(TILES * third, TILES * third + TILES)
+            for n in todo:
+                i, m = divmod(n, k)
+                l = layers[m]
                 nc.tensor.matmul(
                     out=nt[(g, j)][:, P * i : P * i + P],
                     lhsT=normed[(g, l, i)][:, P * j : P * j + P],
                     rhs=ident_f[:],
                     is_transpose=True,
-                    start=(l == 0),
-                    stop=(l == LAYERS - 1),
+                    start=(m == 0),
+                    stop=(m == k - 1),
                 )
 
         def seed(u):
             if not 0 <= u < STEPS:
                 return
             g, j, t = split_unit(u)
-            rest = rest2 if on_scalar(u) else rest3
-            acc[u] = stage.tile([P, TILES * P], F32, bufs=6, name="acc")
+            rest = rest2 if scalar_layers(u) else rest3
+            acc[u] = stage.tile([P, TILES * P], F32, bufs=12, name="acc")
             nc.scalar.activation(
                 out=acc[u][:], in_=nt[(g, j)][:], func=ACT.Identity,
                 scale=gain[:, t, j : j + 1], bias=rest[:, t, j : j + 1],
@@ -292,7 +328,7 @@ def tile_dcadecoderblock_pa_t_kernel(
         def product(u, l):
             g, j, t = split_unit(u)
             cols = slice(P * j, P * j + P)
-            prod = psum.tile([P, TILES * P], F32, tag="prod", bufs=3, name="prod")
+            prod = psum.tile([P, TILES * P], F32, tag="prod", bufs=NP, name="prod")
             nc.tensor.matmul_mx(
                 out=prod[:],
                 lhsT=w_codes[t][:, cols].bitcast(FP8X4),
@@ -302,10 +338,10 @@ def tile_dcadecoderblock_pa_t_kernel(
                 start=True,
                 stop=True,
             )
-            if l == LAYERS - 1 and on_scalar(u):
-                relued[u] = stage.tile([P, TILES * P], F32, bufs=4, name="relued")
+            if on_scalar(u, l):
+                relued[(u, l)] = stage.tile([P, TILES * P], F32, bufs=RB, name="relued")
                 nc.scalar.activation(
-                    out=relued[u][:], in_=prod[:], func=ACT.Relu, bias=bias[:, t, j : j + 1], scale=1.0
+                    out=relued[(u, l)][:], in_=prod[:], func=ACT.Relu, bias=bias[:, t, j : j + 1], scale=1.0
                 )
             else:
                 nc.vector.scalar_tensor_tensor(
@@ -317,8 +353,8 @@ def tile_dcadecoderblock_pa_t_kernel(
             if not 0 <= u < STEPS:
                 return
             g, j, t = split_unit(u)
-            parts = [acc[u], relued[u]] if on_scalar(u) else [acc[u]]
-            turned = psum.tile([P, TILES, P], F32, tag="back", bufs=2, name="turned")
+            parts = [acc[u]] + [relued[(u, l)] for l in scalar_layers(u)]
+            turned = psum.tile([P, TILES, P], F32, tag="back", bufs=NB, name="turned")
             for i in range(TILES):
                 for n, part in enumerate(parts):
                     nc.tensor.matmul(
@@ -333,45 +369,37 @@ def tile_dcadecoderblock_pa_t_kernel(
             nc.scalar.copy(out=result[:], in_=turned[:])
             nc.sync.dma_start(out=rows_of_group(outs[t], g)[:, :, P * j : P * j + P], in_=result[:])
 
-        warm = small.tile([P, 1], F32, name="warm")
-        nc.scalar.activation(out=warm[:], in_=eps[:], func=ACT.Sqrt, bias=eps[:], scale=1.0)
-
         def layer_statistics(l):
             for i in range(TILES):
                 statistics(TILES * l + i)
-            moments(TILES * l + TILES - 1, nc.vector)
-
-        def layer_scale(l):
-            deviation(TILES * l)
-            reciprocal(TILES * l)
+            moments(TILES * l + TILES - 1)
             for i in range(TILES):
                 scale(TILES * l + i)
 
+        def layer_x(l):
+            for h in range(2):
+                transpose_x(2 * l + h)
+
+        def layer_quantise(l):
+            for h in range(2):
+                quantise_x(2 * l + h)
+
+        layer_x(0)
         layer_statistics(0)
-        transpose_x(0)
-        transpose_x(1)
-        quantise_x(0)
-        quantise_x(1)
+        layer_quantise(0)
         regroup_weight(0, 0)
-        layer_scale(0)
         regroup_weight(0, 1)
+        layer_x(1)
         layer_statistics(1)
-        transpose_x(2)
-        transpose_x(3)
-        quantise_x(2)
-        quantise_x(3)
+        layer_quantise(1)
         regroup_weight(1, 0)
-        layer_scale(1)
         regroup_weight(1, 1)
-        layer_statistics(2)
-        transpose_x(4)
-        transpose_x(5)
         quantise_weight(0)
-        quantise_x(4)
-        quantise_x(5)
-        layer_scale(2)
-        constants()
+        layer_x(2)
+        layer_statistics(2)
+        layer_quantise(2)
         quantise_weight(1)
+        constants()
         regroup_weight(2, 0)
         regroup_weight(2, 1)
 
@@ -383,30 +411,23 @@ def tile_dcadecoderblock_pa_t_kernel(
             live = 0 <= u < STEPS
             odd = u % 2 == 1
             if live:
-                product(u, 0)
-            if odd:
+                base, l = u - u % 3, u % 3
+                order = sorted(range(KINDS), key=lambda t: ORD[0] if on_scalar(base + t, l) else t)
+                for t in order:
+                    product(base + t, l)
+            if (u + LEAD_QUANTISE) % 2 == 0:
                 after_first(u + LEAD_QUANTISE, quantise_x, (u + LEAD_QUANTISE) // 2)
-            else:
-                after_first(u + LEAD_STATS, statistics, u + LEAD_STATS)
-            if live and on_scalar(u):
-                product(u, 2)
-            if live:
-                product(u, 1)
-            if odd:
-                after_first(u + LEAD_STATS, statistics, u + LEAD_STATS)
-            if live and not on_scalar(u):
-                product(u, 2)
+            after_first(u + LEAD_STATS, statistics, u + LEAD_STATS)
+            seed(u + LEAD_SEED)
             back(u - LAG_BACK)
             fill_nt(u + LEAD_FILL)
-            seed(u + LEAD_SEED)
-            if odd:
+            s_second(u + LEAD_STATS - 1)
+            if (u + LEAD_XT) % 2 == 0:
                 after_first(u + LEAD_XT, transpose_x, (u + LEAD_XT) // 2)
             if u == -1:
                 quantise_weight(2)
-            after_first(u + LEAD_SCALE, deviation, u + LEAD_SCALE)
-            after_first(u + LEAD_SCALE, reciprocal, u + LEAD_SCALE)
             m, within = divmod(u + LEAD_SCALE, TILES)
             if within < 2:
                 after_first(TILES * m, scale, TILES * m + 2 * within)
                 after_first(TILES * m, scale, TILES * m + 2 * within + 1)
-            after_first(u + LEAD_STATS, moments, u + LEAD_STATS, nc.gpsimd)
+            after_first(u + LEAD_STATS, moments, u + LEAD_STATS)

@@ -27,16 +27,20 @@ PAIRS = STEPS // 2
 
 LEAD_SEED = 3
 LEAD_FILL = 6
-LEAD_XT = 14
+LEAD_XT = 16
 LEAD_QUANTISE = 12
-LEAD_SCALE = 15
-LEAD_STATS = 19
+LEAD_SCALE = 16
+LEAD_STATS = 21
 LAG_BACK = 3
 ON_S = ((0,0,0),(0,2,2),(1,1,1))
 RB = 6
 ORD = (0.5,)
-S_TILES = ()
+S_TILES = (3,)
 YS = 0
+LASTF = 36
+ON_L = ()
+G0Y = (0, 1, 2)
+LEAD_DEV = 16
 NP, NN, NB = 3, 2, 2
 VORD = 'a'
 
@@ -98,14 +102,15 @@ def tile_dcadecoderblock_pa_t_kernel(
         make_identity(nc, ident_f[:])
         ident_b = keep.tile([P, P], BF16, name="ident_b")
         make_identity(nc, ident_b[:])
-        power = keep.tile([P, TILES], F32, name="power")
-        nc.vector.memset(power[:], -0.5)
+        eps = keep.tile([P, 1], F32, name="eps")
+        nc.vector.memset(eps[:], EPS)
 
         vec_cols = keep.tile([P, KINDS, 3, BLOCKS], F32, name="vec_cols")
         bias = vec_cols[:, :, 0, :]
         gain = vec_cols[:, :, 1, :]
         shift = vec_cols[:, :, 2, :]
         neg_bias = keep.tile([P, KINDS, BLOCKS], F32, name="neg_bias")
+        both_vec = keep.tile([P, KINDS, BLOCKS], F32, name="both_vec")
         rest2 = keep.tile([P, KINDS, BLOCKS], F32, name="rest2")
         rest3 = keep.tile([P, KINDS, BLOCKS], F32, name="rest3")
 
@@ -120,6 +125,8 @@ def tile_dcadecoderblock_pa_t_kernel(
             return g, l, i
 
         def on_scalar(u, l):
+            if u >= LASTF:
+                return (u // 3 % 2, u % 3, l) in ON_L
             return (u // 3 % 2, u % 3, l) in ON_S
 
         def scalar_layers(u):
@@ -128,17 +135,14 @@ def tile_dcadecoderblock_pa_t_kernel(
         def constants():
             vec_ps = psum.tile([P, P], BF16, tag="xt", name="vec_ps")
             nc.tensor.transpose(vec_ps[:], vec_rows[:], ident_b[:])
-            nc.vector.tensor_copy(
+            nc.scalar.copy(
                 out=vec_cols[:].rearrange("p t v j -> p (t v j)"), in_=vec_ps[:, 0 : KINDS * 3 * BLOCKS]
             )
-            nc.vector.tensor_scalar_mul(out=neg_bias[:], in0=bias, scalar1=-1.0)
-            nc.vector.tensor_scalar_mul(out=rest2[:], in0=shift, scalar1=3.0)
-            nc.vector.scalar_tensor_tensor(
-                out=rest3[:], in0=bias, scalar=3.0, in1=rest2[:], op0=ALU.mult, op1=ALU.add
-            )
-            nc.vector.scalar_tensor_tensor(
-                out=rest2[:], in0=bias, scalar=2.0, in1=rest2[:], op0=ALU.mult, op1=ALU.add
-            )
+            pool = nc.gpsimd
+            pool.tensor_scalar(out=neg_bias[:], in0=bias, scalar1=-1.0, scalar2=0.0, op0=ALU.mult, op1=ALU.add)
+            pool.tensor_tensor(out=both_vec[:], in0=bias, in1=shift, op=ALU.add)
+            pool.tensor_scalar(out=rest3[:], in0=both_vec[:], scalar1=3.0, scalar2=0.0, op0=ALU.mult, op1=ALU.add)
+            pool.tensor_tensor(out=rest2[:], in0=rest3[:], in1=neg_bias[:], op=ALU.add)
 
         w_grouped = {}
         w_codes = {}
@@ -146,7 +150,7 @@ def tile_dcadecoderblock_pa_t_kernel(
 
         def regroup_weight(t, half):
             if half == 0:
-                w_grouped[t] = stage.tile([P, D, PACK], BF16, align_bytes=64, name="w_grouped")
+                w_grouped[t] = stage.tile([P, D, PACK], BF16, align_bytes=64, bufs=3, name="w_grouped")
             cols = slice(D // 2 * half, D // 2 * half + D // 2)
             nc.scalar.copy(
                 out=w_grouped[t][:, cols, :].rearrange("p (c i) t -> p c t i", i=4),
@@ -202,6 +206,8 @@ def tile_dcadecoderblock_pa_t_kernel(
         total = {}
         neg_mean = {}
         rstd = {}
+        mean_var = {}
+        neg_rstd = {}
         offset = {}
 
         def statistics(s):
@@ -215,61 +221,71 @@ def tile_dcadecoderblock_pa_t_kernel(
             else:
                 nc.vector.bn_stats(out=stats[(g, l)][:, i, :], in_=x_sb[(g, l)][:, i, :])
 
-        s_sum = {}
-        s_tot = {}
-        s_neg = {}
+        squares = {}
 
         def s_first(g, l, i):
+            ensure(g, l)
             junk = stage.tile([P, D], BF16, name="junk")
-            s_sum[(g, l, i)] = small.tile([P, 1], F32, name="s_sum")
-            nc.scalar.activation(out=junk[:], in_=x_sb[(g, l)][:, i, :], func=ACT.Identity, accum_out=s_sum[(g, l, i)][:])
-            s_neg[(g, l, i)] = small.tile([P, 1], F32, name="s_neg")
-            nc.gpsimd.tensor_scalar(out=s_neg[(g, l, i)][:], in0=s_sum[(g, l, i)][:], scalar1=-1.0 / D, scalar2=0.0, op0=ALU.mult, op1=ALU.add)
+            nc.scalar.activation(
+                out=junk[:], in_=x_sb[(g, l)][:, i, :], func=ACT.Identity, bias=0.0, scale=1.0 / D,
+                accum_out=mean_var[(g, l)][:, i, 0:1],
+            )
 
         def s_second(s):
-            if not 0 <= s < STEPS:
-                return
             g, l, i = split_tile(s)
             if g > 0 and i in S_TILES:
                 junk = stage.tile([P, D], BF16, name="junk")
-                s_tot[(g, l, i)] = small.tile([P, 1], F32, name="s_tot")
-                nc.scalar.activation(out=junk[:], in_=x_sb[(g, l)][:, i, :], func=ACT.Square, bias=s_neg[(g, l, i)][:], accum_out=s_tot[(g, l, i)][:])
+                squares[(g, l)] = small.tile([P, 1], F32, name="squares")
+                nc.scalar.activation(
+                    out=junk[:], in_=x_sb[(g, l)][:, i, :], func=ACT.Square, scale=-1.0,
+                    bias=mean_var[(g, l)][:, i, 0:1], accum_out=squares[(g, l)][:],
+                )
 
-        def moments(s):
-            if s >= STEPS or s % TILES != TILES - 1:
+        def ensure(g, l):
+            if (g, l) not in mean_var:
+                mean_var[(g, l)] = small.tile([P, TILES, 2], F32, name="mean_var")
+
+        def aggregate(s):
+            if s >= STEPS:
                 return
             g, l, i = split_tile(s)
-            st = stats[(g, l)]
-            diff = small.tile([P, TILES], F32, name="diff")
-            half = small.tile([P, TILES], F32, name="half")
-            both = small.tile([P, TILES], F32, name="both")
-            var = small.tile([P, TILES], F32, name="var")
-            mean2 = small.tile([P, TILES], F32, name="mean2")
-            neg_mean = small.tile([P, TILES], F32, name="neg_mean")
+            ensure(g, l)
+            if g > 0 and i in S_TILES:
+                return
+            nc.vector.bn_aggr(out=mean_var[(g, l)][:, i, :], in_=stats[(g, l)][:, i, :])
+
+        def deviation(s):
+            if s >= STEPS or s % TILES:
+                return
+            g, l, i = split_tile(s)
             rstd[(g, l)] = small.tile([P, TILES], F32, name="rstd")
+            neg_rstd[(g, l)] = small.tile([P, TILES], F32, name="neg_rstd")
+            n = TILES - len(S_TILES) if g > 0 else TILES
+            nc.scalar.activation(
+                out=rstd[(g, l)][:, :n], in_=mean_var[(g, l)][:, :n, 1], func=ACT.Abs_reciprocal_sqrt, bias=eps[:], scale=1.0
+            )
+            if n < TILES:
+                nc.scalar.activation(
+                    out=rstd[(g, l)][:, n:], in_=squares[(g, l)][:], func=ACT.Abs_reciprocal_sqrt, bias=eps[:], scale=1.0 / D
+                )
+            nc.scalar.mul(out=neg_rstd[(g, l)][:], in_=rstd[(g, l)][:], mul=-1.0)
+
+        def offsets(s):
+            if s >= STEPS or s % TILES:
+                return
+            g, l, i = split_tile(s)
             offset[(g, l)] = small.tile([P, TILES], F32, name="offset")
-            pool = nc.gpsimd
-            pool.tensor_tensor(out=diff[:], in0=st[:, :, 1], in1=st[:, :, 4], op=ALU.subtract)
-            pool.tensor_tensor(out=both[:], in0=st[:, :, 2], in1=st[:, :, 5], op=ALU.add)
-            pool.tensor_scalar(
-                out=half[:], in0=diff[:], scalar1=float(D // 4), scalar2=0.0, op0=ALU.mult, op1=ALU.add
+            nc.gpsimd.tensor_tensor(
+                out=offset[(g, l)][:], in0=mean_var[(g, l)][:, :, 0], in1=neg_rstd[(g, l)][:], op=ALU.mult
             )
-            pool.tensor_tensor(out=half[:], in0=half[:], in1=diff[:], op=ALU.mult)
-            pool.tensor_tensor(out=var[:], in0=half[:], in1=both[:], op=ALU.add)
-            pool.tensor_scalar(out=var[:], in0=var[:], scalar1=1.0 / D, scalar2=EPS, op0=ALU.mult, op1=ALU.add)
-            pool.tensor_tensor(out=rstd[(g, l)][:], in0=var[:], in1=power[:], op=ALU.pow)
-            pool.tensor_tensor(out=mean2[:], in0=st[:, :, 1], in1=st[:, :, 4], op=ALU.add)
-            pool.tensor_scalar(
-                out=neg_mean[:], in0=mean2[:], scalar1=-0.5, scalar2=0.0, op0=ALU.mult, op1=ALU.add
-            )
-            pool.tensor_tensor(out=offset[(g, l)][:], in0=neg_mean[:], in1=rstd[(g, l)][:], op=ALU.mult)
 
         def scale(s):
             if s >= STEPS:
                 return
             g, l, i = split_tile(s)
             y = stage.tile([P, D], F32, bufs=2 * LAYERS * TILES, name="normed")
-            nc.gpsimd.tensor_scalar(
+            engine = nc.vector if g == 0 and l in G0Y else nc.gpsimd
+            engine.tensor_scalar(
                 out=y[:], in0=x_sb[(g, l)][:, i, :],
                 scalar1=rstd[(g, l)][:, i : i + 1], scalar2=offset[(g, l)][:, i : i + 1],
                 op0=ALU.mult, op1=ALU.add,
@@ -369,10 +385,18 @@ def tile_dcadecoderblock_pa_t_kernel(
             nc.scalar.copy(out=result[:], in_=turned[:])
             nc.sync.dma_start(out=rows_of_group(outs[t], g)[:, :, P * j : P * j + P], in_=result[:])
 
+        warm = small.tile([P, 1], F32, name="warm")
+        nc.scalar.activation(out=warm[:], in_=eps[:], func=ACT.Abs_reciprocal_sqrt, bias=eps[:], scale=1.0)
+
         def layer_statistics(l):
             for i in range(TILES):
                 statistics(TILES * l + i)
-            moments(TILES * l + TILES - 1)
+                if i > 0:
+                    aggregate(TILES * l + i - 1)
+            aggregate(TILES * l + TILES - 1)
+
+        def layer_norm(l):
+            offsets(TILES * l)
             for i in range(TILES):
                 scale(TILES * l + i)
 
@@ -384,22 +408,28 @@ def tile_dcadecoderblock_pa_t_kernel(
             for h in range(2):
                 quantise_x(2 * l + h)
 
-        layer_x(0)
         layer_statistics(0)
-        layer_quantise(0)
+        layer_x(0)
         regroup_weight(0, 0)
+        deviation(0)
+        layer_statistics(1)
+        layer_norm(0)
         regroup_weight(0, 1)
         layer_x(1)
-        layer_statistics(1)
-        layer_quantise(1)
+        layer_quantise(0)
+        deviation(TILES)
         regroup_weight(1, 0)
-        regroup_weight(1, 1)
-        quantise_weight(0)
-        layer_x(2)
         layer_statistics(2)
+        layer_norm(1)
+        layer_quantise(1)
+        quantise_weight(0)
+        regroup_weight(1, 1)
+        layer_x(2)
+        deviation(2 * TILES)
+        layer_norm(2)
+        constants()
         layer_quantise(2)
         quantise_weight(1)
-        constants()
         regroup_weight(2, 0)
         regroup_weight(2, 1)
 
@@ -418,16 +448,19 @@ def tile_dcadecoderblock_pa_t_kernel(
             if (u + LEAD_QUANTISE) % 2 == 0:
                 after_first(u + LEAD_QUANTISE, quantise_x, (u + LEAD_QUANTISE) // 2)
             after_first(u + LEAD_STATS, statistics, u + LEAD_STATS)
+            after_first(u + LEAD_STATS - 1, aggregate, u + LEAD_STATS - 1)
+            if u + LEAD_STATS - 1 < STEPS:
+                after_first(u + LEAD_STATS - 1, s_second, u + LEAD_STATS - 1)
             seed(u + LEAD_SEED)
             back(u - LAG_BACK)
             fill_nt(u + LEAD_FILL)
-            s_second(u + LEAD_STATS - 1)
             if (u + LEAD_XT) % 2 == 0:
                 after_first(u + LEAD_XT, transpose_x, (u + LEAD_XT) // 2)
             if u == -1:
                 quantise_weight(2)
+            after_first(u + LEAD_DEV, deviation, u + LEAD_DEV)
+            after_first(u + LEAD_SCALE, offsets, u + LEAD_SCALE)
             m, within = divmod(u + LEAD_SCALE, TILES)
             if within < 2:
                 after_first(TILES * m, scale, TILES * m + 2 * within)
                 after_first(TILES * m, scale, TILES * m + 2 * within + 1)
-            after_first(u + LEAD_STATS, moments, u + LEAD_STATS)

@@ -1,3 +1,4 @@
+import math
 from contextlib import ExitStack
 
 import concourse.mybir as mybir
@@ -26,22 +27,47 @@ PER_GROUP = BLOCKS * KINDS
 PAIRS = STEPS // 2
 
 LEAD_SEED = 3
-LEAD_FILL = 6
+LEAD_FILL = 5
 LEAD_XT = 16
 LEAD_QUANTISE = 12
 LEAD_SCALE = 16
 LEAD_STATS = 21
 LAG_BACK = 3
-ON_S = ((0,0,0),(0,2,2),(1,1,1))
+ON_S = ()
 RB = 6
 ORD = (0.5,)
-S_TILES = (3,)
+S_TILES = (1, 2, 3)
 YS = 0
+EARLY = 0
+AGG = 1
+FILLS = {0: -3, 1: -3, 2: -3, 3: 0, 4: 0, 5: 0, 12: 8, 13: 9, 14: 9}
+SEEDS = {0: -2, 1: -2, 2: -2, 3: 1, 4: 1, 5: 2, 12: 10, 13: 10, 14: 11}
+DEV = 2
+XT_BASE = -1
+XT_RATE = 0.5
+Q_BASE = 1
+Q_RATE = 0.5
+WV_AT = -3
+XP = 9
+PL = 4
+XPS = True
+XB = True
+PSEED = range(48)
+YG = 2
+LS_LATE = 22
+DEVL = 2
+ON_E = ((0, 0, 0), (0, 1, 1), (0, 2, 2), (1, 0, 0), (1, 1, 1), (1, 2, 2))
+S_TILES1 = (2, 3)
+G1_BASE = -7
+G1_RATE = 1
+LEAD_XT1 = 14
+LEAD_QUANTISE1 = 12
+HEAD_STEP = -6
 LASTF = 36
 ON_L = ()
 G0Y = (0, 1, 2)
 LEAD_DEV = 16
-NP, NN, NB = 3, 2, 2
+NP, NN, NB = 5, 1, 2
 VORD = 'a'
 
 FLOPS = 2 * BATCH * LAYERS * SEQ * D * KINDS * D
@@ -125,6 +151,8 @@ def tile_dcadecoderblock_pa_t_kernel(
             return g, l, i
 
         def on_scalar(u, l):
+            if u < EARLY:
+                return (u // 3 % 2, u % 3, l) in ON_E
             if u >= LASTF:
                 return (u // 3 % 2, u % 3, l) in ON_L
             return (u // 3 % 2, u % 3, l) in ON_S
@@ -133,7 +161,7 @@ def tile_dcadecoderblock_pa_t_kernel(
             return [l for l in range(LAYERS) if on_scalar(u, l)]
 
         def constants():
-            vec_ps = psum.tile([P, P], BF16, tag="xt", name="vec_ps")
+            vec_ps = psum.tile([P, P], BF16, tag="nt", bufs=NN, name="vec_ps")
             nc.tensor.transpose(vec_ps[:], vec_rows[:], ident_b[:])
             nc.scalar.copy(
                 out=vec_cols[:].rearrange("p t v j -> p (t v j)"), in_=vec_ps[:, 0 : KINDS * 3 * BLOCKS]
@@ -170,18 +198,33 @@ def tile_dcadecoderblock_pa_t_kernel(
         x_codes = {}
         x_scales = {}
 
+        perms = {}
+
+        def permute_x(q):
+            if q >= PAIRS:
+                return
+            g, l, i = split_tile(2 * q)
+            if g < XP:
+                return
+            words = x_sb[(g, l)][:].bitcast(F32)
+            perms[q] = stage.tile([P, 2, 2, P], F32, bufs=5, name="perm")
+            (nc.scalar.copy if XPS else nc.vector.tensor_copy)(
+                out=perms[q][:], in_=words[:, i : i + 2, :].rearrange("p n (q u) -> p n u q", u=2))
+
         def transpose_x(q):
             if q >= PAIRS:
                 return
             g, l, i = split_tile(2 * q)
             words = x_sb[(g, l)][:].bitcast(F32)
-            if g == 0:
+            if g == 0 or XB:
                 xt = psum.tile([P, 2, 2, P], F32, tag="back", bufs=NB, name="xt")
             else:
                 xt = psum.tile([P, 2, 2, P], F32, tag="xt", name="xt")
+            perm = perms.get(q)
             for n in range(2):
                 for u in range(2):
-                    nc.tensor.transpose(xt[:, n, u, :], words[:, i + n, u : 2 * P : 2], ident_f[:])
+                    src = perm[:, n, u, :] if g >= XP else words[:, i + n, u : 2 * P : 2]
+                    nc.tensor.transpose(xt[:, n, u, :], src, ident_f[:])
             x_grouped[q] = stage.tile([P, 2, P, PACK], BF16, align_bytes=64, bufs=4, name="x_grouped")
             nc.scalar.copy(
                 out=x_grouped[q][:].rearrange("p n r t -> p (n r t)").bitcast(F32).rearrange("p (n r u) -> p n r u", n=2, u=2),
@@ -216,12 +259,15 @@ def tile_dcadecoderblock_pa_t_kernel(
             g, l, i = split_tile(s)
             if i == 0:
                 stats[(g, l)] = small.tile([P, TILES, 6], F32, name="stats")
-            if g > 0 and i in S_TILES:
+            if i in s_tiles(g):
                 s_first(g, l, i)
             else:
                 nc.vector.bn_stats(out=stats[(g, l)][:, i, :], in_=x_sb[(g, l)][:, i, :])
 
         squares = {}
+
+        def s_tiles(g):
+            return (() if g == 0 else S_TILES1 if g == 1 else S_TILES)
 
         def s_first(g, l, i):
             ensure(g, l)
@@ -233,12 +279,13 @@ def tile_dcadecoderblock_pa_t_kernel(
 
         def s_second(s):
             g, l, i = split_tile(s)
-            if g > 0 and i in S_TILES:
+            if i in s_tiles(g):
                 junk = stage.tile([P, D], BF16, name="junk")
-                squares[(g, l)] = small.tile([P, 1], F32, name="squares")
+                if (g, l) not in squares:
+                    squares[(g, l)] = small.tile([P, TILES], F32, name="squares")
                 nc.scalar.activation(
                     out=junk[:], in_=x_sb[(g, l)][:, i, :], func=ACT.Square, scale=-1.0,
-                    bias=mean_var[(g, l)][:, i, 0:1], accum_out=squares[(g, l)][:],
+                    bias=mean_var[(g, l)][:, i, 0:1], accum_out=squares[(g, l)][:, i : i + 1],
                 )
 
         def ensure(g, l):
@@ -250,7 +297,7 @@ def tile_dcadecoderblock_pa_t_kernel(
                 return
             g, l, i = split_tile(s)
             ensure(g, l)
-            if g > 0 and i in S_TILES:
+            if i in s_tiles(g):
                 return
             nc.vector.bn_aggr(out=mean_var[(g, l)][:, i, :], in_=stats[(g, l)][:, i, :])
 
@@ -260,13 +307,14 @@ def tile_dcadecoderblock_pa_t_kernel(
             g, l, i = split_tile(s)
             rstd[(g, l)] = small.tile([P, TILES], F32, name="rstd")
             neg_rstd[(g, l)] = small.tile([P, TILES], F32, name="neg_rstd")
-            n = TILES - len(S_TILES) if g > 0 else TILES
-            nc.scalar.activation(
+            n = TILES - len(s_tiles(g))
+            if n:
+                nc.scalar.activation(
                 out=rstd[(g, l)][:, :n], in_=mean_var[(g, l)][:, :n, 1], func=ACT.Abs_reciprocal_sqrt, bias=eps[:], scale=1.0
             )
             if n < TILES:
                 nc.scalar.activation(
-                    out=rstd[(g, l)][:, n:], in_=squares[(g, l)][:], func=ACT.Abs_reciprocal_sqrt, bias=eps[:], scale=1.0 / D
+                    out=rstd[(g, l)][:, n:], in_=squares[(g, l)][:, n:], func=ACT.Abs_reciprocal_sqrt, bias=eps[:], scale=1.0 / D
                 )
             nc.scalar.mul(out=neg_rstd[(g, l)][:], in_=rstd[(g, l)][:], mul=-1.0)
 
@@ -291,10 +339,11 @@ def tile_dcadecoderblock_pa_t_kernel(
                 op0=ALU.mult, op1=ALU.add,
             )
             normed[(g, l, i)] = y
-            if g > 0 and 0 < l <= YS:
+            if g >= YG and 0 < l <= YS:
                 nc.gpsimd.tensor_tensor(out=normed[(g, 0, i)][:], in0=normed[(g, 0, i)][:], in1=y[:], op=ALU.add)
 
         nt = {}
+        nts = {}
         acc = {}
 
         def fill_nt(u):
@@ -303,16 +352,15 @@ def tile_dcadecoderblock_pa_t_kernel(
             g, j, third = split_unit(u)
             if third == 0:
                 nt[(g, j)] = psum.tile([P, TILES * P], F32, tag="nt", bufs=NN, name="nt")
-            layers = [0] + [l for l in (1, 2) if l > YS or g == 0]
+            layers = [0] + [l for l in (1, 2) if l > YS or g < YG]
             k = len(layers)
             todo = range(TILES * k)
             if NN == 1:
+                todo = [range(0, 6), range(6, 12), ()][third]
+            elif YS == 2 and g >= YG:
                 if third:
                     return
-            elif YS == 2 and g > 0:
-                if third:
-                    return
-            elif YS == 1 and g > 0:
+            elif YS == 1 and g >= YG:
                 todo = [range(0, 4), range(4, 8), ()][third] if NN > 1 else ([range(8), (), ()][third])
             else:
                 todo = range(TILES * third, TILES * third + TILES)
@@ -333,6 +381,16 @@ def tile_dcadecoderblock_pa_t_kernel(
                 return
             g, j, t = split_unit(u)
             rest = rest2 if scalar_layers(u) else rest3
+            if u in PSEED:
+                if t == 0:
+                    nts[(g, j)] = stage.tile([P, TILES * P], F32, bufs=3, name="nts")
+                    nc.scalar.copy(out=nts[(g, j)][:], in_=nt[(g, j)][:])
+                acc[u] = stage.tile([P, TILES * P], F32, bufs=12, name="acc")
+                nc.gpsimd.tensor_scalar(
+                    out=acc[u][:], in0=nts[(g, j)][:], scalar1=gain[:, t, j : j + 1], scalar2=rest[:, t, j : j + 1],
+                    op0=ALU.mult, op1=ALU.add,
+                )
+                return
             acc[u] = stage.tile([P, TILES * P], F32, bufs=12, name="acc")
             nc.scalar.activation(
                 out=acc[u][:], in_=nt[(g, j)][:], func=ACT.Identity,
@@ -433,34 +491,62 @@ def tile_dcadecoderblock_pa_t_kernel(
         regroup_weight(2, 0)
         regroup_weight(2, 1)
 
-        def after_first(index, work, *arguments):
-            if index >= PER_GROUP:
-                work(*arguments)
+        sched = {}
 
-        for u in range(PER_GROUP - LEAD_STATS, STEPS + LAG_BACK):
+        def put(step, name, fn, *a):
+            sched.setdefault((step, name), []).append((fn, a))
+
+        for s in range(PER_GROUP, STEPS):
+            g = s // PER_GROUP
+            if g == 1:
+                st = math.floor(G1_BASE + (s - PER_GROUP) / G1_RATE)
+            else:
+                st = s - LS_LATE
+            put(st, 'stats', statistics, s)
+            put(st + AGG, 'aggr', aggregate, s)
+            if s % TILES in s_tiles(g):
+                put(st + 1, 'second', s_second, s)
+            if s % TILES == TILES - 1:
+                first = s - TILES + 1
+                d = st + DEV
+                put(d, 'dev', deviation, first)
+                put(d, 'off', offsets, first)
+                for i in range(TILES):
+                    put(d + i // 2, 'scale', scale, first + i)
+        for q in range(PAIRS // GROUPS, PAIRS):
+            one = q < 2 * PAIRS // GROUPS
+            put(math.floor(XT_BASE + (q - 6) / XT_RATE) if one else 2 * q - LEAD_XT, 'xt', transpose_x, q)
+            put(math.floor(Q_BASE + (q - 6) / Q_RATE) if one else 2 * q - LEAD_QUANTISE, 'quant', quantise_x, q)
+        for q in range(12, PAIRS):
+            put(2 * q - LEAD_XT - PL, 'perm', permute_x, q)
+        for u in range(STEPS):
+            put(FILLS.get(u, u - LEAD_FILL), 'fill', fill_nt, u)
+            put(SEEDS.get(u, u - LEAD_SEED), 'seed', seed, u)
+
+        put(WV_AT, 'wv', quantise_weight, 2)
+
+        def do(step, name):
+            for fn, a in sched.pop((step, name), []):
+                fn(*a)
+
+        for u in range(min(k[0] for k in sched), STEPS + LAG_BACK):
             live = 0 <= u < STEPS
-            odd = u % 2 == 1
             if live:
                 base, l = u - u % 3, u % 3
                 order = sorted(range(KINDS), key=lambda t: ORD[0] if on_scalar(base + t, l) else t)
                 for t in order:
                     product(base + t, l)
-            if (u + LEAD_QUANTISE) % 2 == 0:
-                after_first(u + LEAD_QUANTISE, quantise_x, (u + LEAD_QUANTISE) // 2)
-            after_first(u + LEAD_STATS, statistics, u + LEAD_STATS)
-            after_first(u + LEAD_STATS - 1, aggregate, u + LEAD_STATS - 1)
-            if u + LEAD_STATS - 1 < STEPS:
-                after_first(u + LEAD_STATS - 1, s_second, u + LEAD_STATS - 1)
-            seed(u + LEAD_SEED)
+            do(u, 'quant')
+            do(u, 'stats')
+            do(u, 'aggr')
+            do(u, 'second')
+            do(u, 'seed')
+            do(u, 'perm')
             back(u - LAG_BACK)
-            fill_nt(u + LEAD_FILL)
-            if (u + LEAD_XT) % 2 == 0:
-                after_first(u + LEAD_XT, transpose_x, (u + LEAD_XT) // 2)
-            if u == -1:
-                quantise_weight(2)
-            after_first(u + LEAD_DEV, deviation, u + LEAD_DEV)
-            after_first(u + LEAD_SCALE, offsets, u + LEAD_SCALE)
-            m, within = divmod(u + LEAD_SCALE, TILES)
-            if within < 2:
-                after_first(TILES * m, scale, TILES * m + 2 * within)
-                after_first(TILES * m, scale, TILES * m + 2 * within + 1)
+            do(u, 'fill')
+            do(u, 'xt')
+            do(u, 'wv')
+            do(u, 'dev')
+            do(u, 'off')
+            do(u, 'scale')
+        assert not sched, sorted(sched)

@@ -1,4 +1,3 @@
-import math
 from contextlib import ExitStack
 
 import concourse.mybir as mybir
@@ -16,61 +15,52 @@ BATCH, LAYERS, SEQ, D = 2, 3, 1024, 512
 EPS = 1e-5
 P = 128
 PACK = 4
+MX_ALIGN = 256
 TILES = 4
 HALVES = SEQ // (P * TILES)
 GROUPS = BATCH * HALVES
 BLOCKS = D // P
 KINDS = 3
-
-STEPS = GROUPS * BLOCKS * KINDS
-PER_GROUP = BLOCKS * KINDS
+PER_GROUP = BLOCKS * LAYERS
+STEPS = GROUPS * PER_GROUP
 PAIRS = STEPS // 2
 
-LEAD_SEED = 3
-LEAD_FILL = 5
-LEAD_XT = 16
+VECTOR_TILES = 2
+
+LEAD_STATISTICS = 22
+LEAD_STATISTICS_1 = 19
+NORM_AFTER = 2
+LEAD_X = 16
+LEAD_X_1 = 13
 LEAD_QUANTISE = 12
-LEAD_SCALE = 16
-LEAD_STATS = 21
+LEAD_QUANTISE_1 = 11
+LEAD_NT = 6
+LEAD_SEED = 3
 LAG_BACK = 3
-ON_S = ()
-RB = 6
-ORD = (0.5,)
-S_TILES = (1, 2, 3)
-YS = 0
-EARLY = 0
-AGG = 1
-FILLS = {0: -3, 1: -3, 2: -3, 3: 0, 4: 0, 5: 0, 12: 8, 13: 9, 14: 9}
-SEEDS = {0: -2, 1: -2, 2: -2, 3: 1, 4: 1, 5: 2, 12: 10, 13: 10, 14: 11}
-DEV = 2
-XT_BASE = -1
-XT_RATE = 0.5
-Q_BASE = 1
-Q_RATE = 0.5
-WV_AT = -3
-XP = 9
-PL = 4
-XPS = True
-XB = True
-PSEED = range(48)
-YG = 2
-LS_LATE = 22
-DEVL = 2
-ON_E = ((0, 0, 0), (0, 1, 1), (0, 2, 2), (1, 0, 0), (1, 1, 1), (1, 2, 2))
-S_TILES1 = (2, 3)
-G1_BASE = -7
-G1_RATE = 1
-LEAD_XT1 = 14
-LEAD_QUANTISE1 = 12
-HEAD_STEP = -6
-LASTF = 36
-ON_L = ()
-G0Y = (0, 1, 2)
-LEAD_DEV = 16
-NP, NN, NB = 5, 1, 2
-VORD = 'a'
 
 FLOPS = 2 * BATCH * LAYERS * SEQ * D * KINDS * D
+
+
+def nt_step(unit):
+    block, third = divmod(unit, KINDS)
+    if block == 0:
+        return -3
+    if block == 1:
+        return 0
+    if block == BLOCKS:
+        return PER_GROUP - 4 + min(third, 1)
+    return unit - LEAD_NT
+
+
+def seed_step(unit):
+    block, kind = divmod(unit, KINDS)
+    if block == 0:
+        return -2
+    if block == 1:
+        return 1 + kind // 2
+    if block == BLOCKS:
+        return PER_GROUP - 2 + kind // 2
+    return unit - LEAD_SEED
 
 
 def tile_dcadecoderblock_pa_t_kernel(
@@ -91,7 +81,7 @@ def tile_dcadecoderblock_pa_t_kernel(
         keep = stack.enter_context(tc.tile_pool(name="keep", bufs=1))
         stage = stack.enter_context(tc.tile_pool(name="stage", bufs=2))
         small = stack.enter_context(tc.tile_pool(name="small", bufs=4))
-        psum = stack.enter_context(tc.psum_pool(name="psum", bufs=1))
+        psum = stack.enter_context(tc.psum_pool(name="psum", bufs=2))
 
         def rows_of_group(dram, g):
             return dram[g // HALVES].rearrange("(p h i) f -> p h i f", h=HALVES, i=TILES)[:, g % HALVES]
@@ -99,20 +89,18 @@ def tile_dcadecoderblock_pa_t_kernel(
         x_sb = {}
 
         def load_x(g, l):
-            x = keep.tile([P, TILES, D], BF16, name="x%d_%d" % (g, l))
-            nc.sync.dma_start(out=x[:], in_=rows_of_group(layer_outputs[:, l], g))
-            x_sb[(g, l)] = x
+            x_sb[(g, l)] = keep.tile([P, TILES, D], BF16, name="x%d_%d" % (g, l))
+            nc.sync.dma_start(out=x_sb[(g, l)][:], in_=rows_of_group(layer_outputs[:, l], g))
 
         w_raw = {}
 
-        def load_w(t):
-            raw = keep.tile([P, PACK, D], BF16, name="w_raw%d" % t)
-            nc.sync.dma_start(out=raw[:], in_=weights[t].rearrange("(p j) c -> p j c", j=PACK))
-            w_raw[t] = raw
+        def load_weight(t):
+            w_raw[t] = keep.tile([P, PACK, D], BF16, name="w_raw%d" % t)
+            nc.sync.dma_start(out=w_raw[t][:], in_=weights[t].rearrange("(p j) c -> p j c", j=PACK))
 
         for n in range(LAYERS):
             load_x(0, n)
-            load_w(n)
+            load_weight(n)
         vec_rows = keep.tile([P, P], BF16, name="vec_rows")
         nc.vector.memset(vec_rows[:], 0.0)
         for n, vec in enumerate(vectors):
@@ -136,49 +124,43 @@ def tile_dcadecoderblock_pa_t_kernel(
         gain = vec_cols[:, :, 1, :]
         shift = vec_cols[:, :, 2, :]
         neg_bias = keep.tile([P, KINDS, BLOCKS], F32, name="neg_bias")
-        both_vec = keep.tile([P, KINDS, BLOCKS], F32, name="both_vec")
-        rest2 = keep.tile([P, KINDS, BLOCKS], F32, name="rest2")
-        rest3 = keep.tile([P, KINDS, BLOCKS], F32, name="rest3")
+        bias_shift = keep.tile([P, KINDS, BLOCKS], F32, name="bias_shift")
+        rest = keep.tile([P, KINDS, BLOCKS], F32, name="rest")
 
-        def split_unit(u):
-            g, within = divmod(u, BLOCKS * KINDS)
+        def split_unit(unit):
+            g, within = divmod(unit, PER_GROUP)
             j, t = divmod(within, KINDS)
             return g, j, t
 
-        def split_tile(s):
-            g, within = divmod(s, LAYERS * TILES)
+        def split_tile(tile):
+            g, within = divmod(tile, PER_GROUP)
             l, i = divmod(within, TILES)
             return g, l, i
 
-        def on_scalar(u, l):
-            if u < EARLY:
-                return (u // 3 % 2, u % 3, l) in ON_E
-            if u >= LASTF:
-                return (u // 3 % 2, u % 3, l) in ON_L
-            return (u // 3 % 2, u % 3, l) in ON_S
-
-        def scalar_layers(u):
-            return [l for l in range(LAYERS) if on_scalar(u, l)]
-
         def constants():
-            vec_ps = psum.tile([P, P], BF16, tag="nt", bufs=NN, name="vec_ps")
+            vec_ps = psum.tile([P, P], BF16, tag="nt", name="vec_ps")
             nc.tensor.transpose(vec_ps[:], vec_rows[:], ident_b[:])
             nc.scalar.copy(
                 out=vec_cols[:].rearrange("p t v j -> p (t v j)"), in_=vec_ps[:, 0 : KINDS * 3 * BLOCKS]
             )
-            pool = nc.gpsimd
-            pool.tensor_scalar(out=neg_bias[:], in0=bias, scalar1=-1.0, scalar2=0.0, op0=ALU.mult, op1=ALU.add)
-            pool.tensor_tensor(out=both_vec[:], in0=bias, in1=shift, op=ALU.add)
-            pool.tensor_scalar(out=rest3[:], in0=both_vec[:], scalar1=3.0, scalar2=0.0, op0=ALU.mult, op1=ALU.add)
-            pool.tensor_tensor(out=rest2[:], in0=rest3[:], in1=neg_bias[:], op=ALU.add)
+            nc.gpsimd.tensor_scalar(
+                out=neg_bias[:], in0=bias, scalar1=-1.0, scalar2=0.0, op0=ALU.mult, op1=ALU.add
+            )
+            nc.gpsimd.tensor_tensor(out=bias_shift[:], in0=bias, in1=shift, op=ALU.add)
+            nc.gpsimd.tensor_scalar(
+                out=rest[:], in0=bias_shift[:], scalar1=float(LAYERS), scalar2=0.0, op0=ALU.mult, op1=ALU.add
+            )
 
         w_grouped = {}
         w_codes = {}
         w_scales = {}
 
+        def grouped_weight(t):
+            w_grouped[t] = stage.tile([P, D, PACK], BF16, align_bytes=MX_ALIGN, bufs=KINDS, name="w_grouped")
+
         def regroup_weight(t, half):
             if half == 0:
-                w_grouped[t] = stage.tile([P, D, PACK], BF16, align_bytes=64, bufs=3, name="w_grouped")
+                grouped_weight(t)
             cols = slice(D // 2 * half, D // 2 * half + D // 2)
             nc.scalar.copy(
                 out=w_grouped[t][:, cols, :].rearrange("p (c i) t -> p c t i", i=4),
@@ -186,8 +168,8 @@ def tile_dcadecoderblock_pa_t_kernel(
             )
 
         def quantise_weight(t):
-            w_codes[t] = keep.tile([P, D], U32, align_bytes=64, name="w_codes%d" % t)
-            w_scales[t] = keep.tile([P, D], U8, align_bytes=64, name="w_scales%d" % t)
+            w_codes[t] = keep.tile([P, D], U32, align_bytes=MX_ALIGN, name="w_codes%d" % t)
+            w_scales[t] = keep.tile([P, D], U8, align_bytes=MX_ALIGN, name="w_scales%d" % t)
             nc.vector.quantize_mx(
                 out=w_codes[t][:].bitcast(FP8X4),
                 scales=w_scales[t][:],
@@ -198,247 +180,156 @@ def tile_dcadecoderblock_pa_t_kernel(
         x_codes = {}
         x_scales = {}
 
-        perms = {}
-
-        def permute_x(q):
-            if q >= PAIRS:
-                return
-            g, l, i = split_tile(2 * q)
-            if g < XP:
-                return
+        def transpose_x(pair):
+            g, l, i = split_tile(2 * pair)
             words = x_sb[(g, l)][:].bitcast(F32)
-            perms[q] = stage.tile([P, 2, 2, P], F32, bufs=5, name="perm")
-            (nc.scalar.copy if XPS else nc.vector.tensor_copy)(
-                out=perms[q][:], in_=words[:, i : i + 2, :].rearrange("p n (q u) -> p n u q", u=2))
-
-        def transpose_x(q):
-            if q >= PAIRS:
-                return
-            g, l, i = split_tile(2 * q)
-            words = x_sb[(g, l)][:].bitcast(F32)
-            if g == 0 or XB:
-                xt = psum.tile([P, 2, 2, P], F32, tag="back", bufs=NB, name="xt")
-            else:
-                xt = psum.tile([P, 2, 2, P], F32, tag="xt", name="xt")
-            perm = perms.get(q)
+            xt = psum.tile([P, 2, 2, P], F32, tag="back", name="xt")
             for n in range(2):
                 for u in range(2):
-                    src = perm[:, n, u, :] if g >= XP else words[:, i + n, u : 2 * P : 2]
-                    nc.tensor.transpose(xt[:, n, u, :], src, ident_f[:])
-            x_grouped[q] = stage.tile([P, 2, P, PACK], BF16, align_bytes=64, bufs=4, name="x_grouped")
+                    nc.tensor.transpose(xt[:, n, u, :], words[:, i + n, u : 2 * P : 2], ident_f[:])
+            x_grouped[pair] = stage.tile([P, 2, P, PACK], BF16, align_bytes=MX_ALIGN, bufs=4, name="x_grouped")
             nc.scalar.copy(
-                out=x_grouped[q][:].rearrange("p n r t -> p (n r t)").bitcast(F32).rearrange("p (n r u) -> p n r u", n=2, u=2),
+                out=x_grouped[pair][:].rearrange("p n r t -> p (n r t)").bitcast(F32)
+                .rearrange("p (n r u) -> p n r u", n=2, u=2),
                 in_=xt[:].rearrange("p n u r -> p n r u"),
             )
 
-        def quantise_x(q):
-            if q >= PAIRS:
-                return
-            g, l, i = split_tile(2 * q)
+        def quantise_x(pair):
+            g, l, i = split_tile(2 * pair)
             if i == 0:
-                x_codes[(g, l)] = stage.tile([P, TILES * P], U32, align_bytes=64, bufs=6, name="x_codes")
-                x_scales[(g, l)] = stage.tile([P, TILES * P], U8, align_bytes=64, bufs=6, name="x_scales")
+                x_codes[(g, l)] = stage.tile(
+                    [P, TILES * P], U32, align_bytes=MX_ALIGN, bufs=2 * LAYERS, name="x_codes"
+                )
+                x_scales[(g, l)] = stage.tile(
+                    [P, TILES * P], U8, align_bytes=MX_ALIGN, bufs=2 * LAYERS, name="x_scales"
+                )
             nc.vector.quantize_mx(
                 out=x_codes[(g, l)][:, P * i : P * i + 2 * P].bitcast(FP8X4),
                 scales=x_scales[(g, l)][:, P * i : P * i + 2 * P],
-                in_=x_grouped[q][:].rearrange("p n r t -> p (n r t)"),
+                in_=x_grouped[pair][:].rearrange("p n r t -> p (n r t)"),
             )
 
         stats = {}
-        normed = {}
-        total = {}
-        neg_mean = {}
-        rstd = {}
         mean_var = {}
+        squares = {}
+        rstd = {}
         neg_rstd = {}
         offset = {}
+        normed = {}
 
-        def statistics(s):
-            if s >= STEPS:
-                return
-            g, l, i = split_tile(s)
+        def vector_tiles(g):
+            return TILES if g == 0 else VECTOR_TILES
+
+        def statistics(tile):
+            g, l, i = split_tile(tile)
             if i == 0:
                 stats[(g, l)] = small.tile([P, TILES, 6], F32, name="stats")
-            if i in s_tiles(g):
-                s_first(g, l, i)
-            else:
+            if i < vector_tiles(g):
                 nc.vector.bn_stats(out=stats[(g, l)][:, i, :], in_=x_sb[(g, l)][:, i, :])
-
-        squares = {}
-
-        def s_tiles(g):
-            return (() if g == 0 else S_TILES1 if g == 1 else S_TILES)
-
-        def s_first(g, l, i):
-            ensure(g, l)
-            junk = stage.tile([P, D], BF16, name="junk")
-            nc.scalar.activation(
-                out=junk[:], in_=x_sb[(g, l)][:, i, :], func=ACT.Identity, bias=0.0, scale=1.0 / D,
-                accum_out=mean_var[(g, l)][:, i, 0:1],
-            )
-
-        def s_second(s):
-            g, l, i = split_tile(s)
-            if i in s_tiles(g):
+            else:
                 junk = stage.tile([P, D], BF16, name="junk")
-                if (g, l) not in squares:
+                nc.scalar.activation(
+                    out=junk[:], in_=x_sb[(g, l)][:, i, :], func=ACT.Identity, bias=0.0, scale=1.0 / D,
+                    accum_out=mean_var[(g, l)][:, i, 0:1],
+                )
+
+        def spread(tile):
+            g, l, i = split_tile(tile)
+            if i == 0:
+                mean_var[(g, l)] = small.tile([P, TILES, 2], F32, name="mean_var")
+            if i < vector_tiles(g):
+                nc.vector.bn_aggr(out=mean_var[(g, l)][:, i, :], in_=stats[(g, l)][:, i, :])
+            else:
+                junk = stage.tile([P, D], BF16, name="junk")
+                if i == vector_tiles(g):
                     squares[(g, l)] = small.tile([P, TILES], F32, name="squares")
                 nc.scalar.activation(
                     out=junk[:], in_=x_sb[(g, l)][:, i, :], func=ACT.Square, scale=-1.0,
                     bias=mean_var[(g, l)][:, i, 0:1], accum_out=squares[(g, l)][:, i : i + 1],
                 )
 
-        def ensure(g, l):
-            if (g, l) not in mean_var:
-                mean_var[(g, l)] = small.tile([P, TILES, 2], F32, name="mean_var")
-
-        def aggregate(s):
-            if s >= STEPS:
-                return
-            g, l, i = split_tile(s)
-            ensure(g, l)
-            if i in s_tiles(g):
-                return
-            nc.vector.bn_aggr(out=mean_var[(g, l)][:, i, :], in_=stats[(g, l)][:, i, :])
-
-        def deviation(s):
-            if s >= STEPS or s % TILES:
-                return
-            g, l, i = split_tile(s)
+        def deviation(g, l):
             rstd[(g, l)] = small.tile([P, TILES], F32, name="rstd")
             neg_rstd[(g, l)] = small.tile([P, TILES], F32, name="neg_rstd")
-            n = TILES - len(s_tiles(g))
-            if n:
-                nc.scalar.activation(
-                out=rstd[(g, l)][:, :n], in_=mean_var[(g, l)][:, :n, 1], func=ACT.Abs_reciprocal_sqrt, bias=eps[:], scale=1.0
+            n = vector_tiles(g)
+            nc.scalar.activation(
+                out=rstd[(g, l)][:, :n], in_=mean_var[(g, l)][:, :n, 1],
+                func=ACT.Abs_reciprocal_sqrt, bias=eps[:], scale=1.0,
             )
             if n < TILES:
                 nc.scalar.activation(
-                    out=rstd[(g, l)][:, n:], in_=squares[(g, l)][:, n:], func=ACT.Abs_reciprocal_sqrt, bias=eps[:], scale=1.0 / D
+                    out=rstd[(g, l)][:, n:], in_=squares[(g, l)][:, n:],
+                    func=ACT.Abs_reciprocal_sqrt, bias=eps[:], scale=1.0 / D,
                 )
             nc.scalar.mul(out=neg_rstd[(g, l)][:], in_=rstd[(g, l)][:], mul=-1.0)
 
-        def offsets(s):
-            if s >= STEPS or s % TILES:
-                return
-            g, l, i = split_tile(s)
+        def offsets(g, l):
             offset[(g, l)] = small.tile([P, TILES], F32, name="offset")
             nc.gpsimd.tensor_tensor(
                 out=offset[(g, l)][:], in0=mean_var[(g, l)][:, :, 0], in1=neg_rstd[(g, l)][:], op=ALU.mult
             )
 
-        def scale(s):
-            if s >= STEPS:
-                return
-            g, l, i = split_tile(s)
-            y = stage.tile([P, D], F32, bufs=2 * LAYERS * TILES, name="normed")
-            engine = nc.vector if g == 0 and l in G0Y else nc.gpsimd
+        def normalise(g, l, i):
+            y = stage.tile([P, D], F32, bufs=2 * PER_GROUP, name="normed")
+            engine = nc.vector if g == 0 and l > 0 else nc.gpsimd
             engine.tensor_scalar(
                 out=y[:], in0=x_sb[(g, l)][:, i, :],
                 scalar1=rstd[(g, l)][:, i : i + 1], scalar2=offset[(g, l)][:, i : i + 1],
                 op0=ALU.mult, op1=ALU.add,
             )
             normed[(g, l, i)] = y
-            if g >= YG and 0 < l <= YS:
-                nc.gpsimd.tensor_tensor(out=normed[(g, 0, i)][:], in0=normed[(g, 0, i)][:], in1=y[:], op=ALU.add)
 
         nt = {}
-        nts = {}
         acc = {}
 
-        def fill_nt(u):
-            if not 0 <= u < STEPS:
-                return
-            g, j, third = split_unit(u)
+        def transpose_normed(unit):
+            g, j, third = split_unit(unit)
             if third == 0:
-                nt[(g, j)] = psum.tile([P, TILES * P], F32, tag="nt", bufs=NN, name="nt")
-            layers = [0] + [l for l in (1, 2) if l > YS or g < YG]
-            k = len(layers)
-            todo = range(TILES * k)
-            if NN == 1:
-                todo = [range(0, 6), range(6, 12), ()][third]
-            elif YS == 2 and g >= YG:
-                if third:
-                    return
-            elif YS == 1 and g >= YG:
-                todo = [range(0, 4), range(4, 8), ()][third] if NN > 1 else ([range(8), (), ()][third])
-            else:
-                todo = range(TILES * third, TILES * third + TILES)
-            for n in todo:
-                i, m = divmod(n, k)
-                l = layers[m]
+                nt[(g, j)] = psum.tile([P, TILES * P], F32, tag="nt", name="nt")
+            for n in range(TILES * third, TILES * third + TILES):
+                i, l = divmod(n, LAYERS)
                 nc.tensor.matmul(
                     out=nt[(g, j)][:, P * i : P * i + P],
                     lhsT=normed[(g, l, i)][:, P * j : P * j + P],
                     rhs=ident_f[:],
                     is_transpose=True,
-                    start=(m == 0),
-                    stop=(m == k - 1),
+                    start=(l == 0),
+                    stop=(l == LAYERS - 1),
                 )
 
-        def seed(u):
-            if not 0 <= u < STEPS:
-                return
-            g, j, t = split_unit(u)
-            rest = rest2 if scalar_layers(u) else rest3
-            if u in PSEED:
-                if t == 0:
-                    nts[(g, j)] = stage.tile([P, TILES * P], F32, bufs=3, name="nts")
-                    nc.scalar.copy(out=nts[(g, j)][:], in_=nt[(g, j)][:])
-                acc[u] = stage.tile([P, TILES * P], F32, bufs=12, name="acc")
-                nc.gpsimd.tensor_scalar(
-                    out=acc[u][:], in0=nts[(g, j)][:], scalar1=gain[:, t, j : j + 1], scalar2=rest[:, t, j : j + 1],
-                    op0=ALU.mult, op1=ALU.add,
-                )
-                return
-            acc[u] = stage.tile([P, TILES * P], F32, bufs=12, name="acc")
+        def seed(unit):
+            g, j, t = split_unit(unit)
+            acc[unit] = stage.tile([P, TILES * P], F32, bufs=12, name="acc")
             nc.scalar.activation(
-                out=acc[u][:], in_=nt[(g, j)][:], func=ACT.Identity,
+                out=acc[unit][:], in_=nt[(g, j)][:], func=ACT.Identity,
                 scale=gain[:, t, j : j + 1], bias=rest[:, t, j : j + 1],
             )
 
-        relued = {}
-
-        def product(u, l):
-            g, j, t = split_unit(u)
+        def products(step):
+            g, j, l = split_unit(step)
             cols = slice(P * j, P * j + P)
-            prod = psum.tile([P, TILES * P], F32, tag="prod", bufs=NP, name="prod")
-            nc.tensor.matmul_mx(
-                out=prod[:],
-                lhsT=w_codes[t][:, cols].bitcast(FP8X4),
-                lhsT_scale=w_scales[t][:, cols],
-                rhs=x_codes[(g, l)][:].bitcast(FP8X4),
-                rhs_scale=x_scales[(g, l)][:],
-                start=True,
-                stop=True,
-            )
-            if on_scalar(u, l):
-                relued[(u, l)] = stage.tile([P, TILES * P], F32, bufs=RB, name="relued")
-                nc.scalar.activation(
-                    out=relued[(u, l)][:], in_=prod[:], func=ACT.Relu, bias=bias[:, t, j : j + 1], scale=1.0
+            for t in range(KINDS):
+                unit = step - l + t
+                prod = psum.tile([P, TILES * P], F32, tag="prod", bufs=4, name="prod")
+                nc.tensor.matmul_mx(
+                    out=prod[:],
+                    lhsT=w_codes[t][:, cols].bitcast(FP8X4),
+                    lhsT_scale=w_scales[t][:, cols],
+                    rhs=x_codes[(g, l)][:].bitcast(FP8X4),
+                    rhs_scale=x_scales[(g, l)][:],
+                    start=True,
+                    stop=True,
                 )
-            else:
                 nc.vector.scalar_tensor_tensor(
-                    out=acc[u][:], in0=prod[:], scalar=neg_bias[:, t, j : j + 1],
-                    in1=acc[u][:], op0=ALU.max, op1=ALU.add,
+                    out=acc[unit][:], in0=prod[:], scalar=neg_bias[:, t, j : j + 1],
+                    in1=acc[unit][:], op0=ALU.max, op1=ALU.add,
                 )
 
-        def back(u):
-            if not 0 <= u < STEPS:
-                return
-            g, j, t = split_unit(u)
-            parts = [acc[u]] + [relued[(u, l)] for l in scalar_layers(u)]
-            turned = psum.tile([P, TILES, P], F32, tag="back", bufs=NB, name="turned")
+        def back(unit):
+            g, j, t = split_unit(unit)
+            turned = psum.tile([P, TILES, P], F32, tag="back", name="turned")
             for i in range(TILES):
-                for n, part in enumerate(parts):
-                    nc.tensor.matmul(
-                        out=turned[:, i, :],
-                        lhsT=part[:, P * i : P * i + P],
-                        rhs=ident_f[:],
-                        is_transpose=True,
-                        start=(n == 0),
-                        stop=(n == len(parts) - 1),
-                    )
+                nc.tensor.transpose(turned[:, i, :], acc[unit][:, P * i : P * i + P], ident_f[:])
             result = stage.tile([P, TILES, P], F32, bufs=4, name="result")
             nc.scalar.copy(out=result[:], in_=turned[:])
             nc.sync.dma_start(out=rows_of_group(outs[t], g)[:, :, P * j : P * j + P], in_=result[:])
@@ -447,43 +338,44 @@ def tile_dcadecoderblock_pa_t_kernel(
         nc.scalar.activation(out=warm[:], in_=eps[:], func=ACT.Abs_reciprocal_sqrt, bias=eps[:], scale=1.0)
 
         def layer_statistics(l):
-            for i in range(TILES):
-                statistics(TILES * l + i)
-                if i > 0:
-                    aggregate(TILES * l + i - 1)
-            aggregate(TILES * l + TILES - 1)
+            first = TILES * l
+            for tile in range(first, first + TILES):
+                statistics(tile)
+                if tile > first:
+                    spread(tile - 1)
+            spread(first + TILES - 1)
 
         def layer_norm(l):
-            offsets(TILES * l)
+            offsets(0, l)
             for i in range(TILES):
-                scale(TILES * l + i)
+                normalise(0, l, i)
 
-        def layer_x(l):
-            for h in range(2):
-                transpose_x(2 * l + h)
+        def layer_transposes(l):
+            for pair in (2 * l, 2 * l + 1):
+                transpose_x(pair)
 
         def layer_quantise(l):
-            for h in range(2):
-                quantise_x(2 * l + h)
+            for pair in (2 * l, 2 * l + 1):
+                quantise_x(pair)
 
         layer_statistics(0)
-        layer_x(0)
+        layer_transposes(0)
         regroup_weight(0, 0)
-        deviation(0)
+        deviation(0, 0)
         layer_statistics(1)
         layer_norm(0)
         regroup_weight(0, 1)
-        layer_x(1)
+        layer_transposes(1)
         layer_quantise(0)
-        deviation(TILES)
+        deviation(0, 1)
         regroup_weight(1, 0)
         layer_statistics(2)
         layer_norm(1)
         layer_quantise(1)
         quantise_weight(0)
         regroup_weight(1, 1)
-        layer_x(2)
-        deviation(2 * TILES)
+        layer_transposes(2)
+        deviation(0, 2)
         layer_norm(2)
         constants()
         layer_quantise(2)
@@ -491,62 +383,39 @@ def tile_dcadecoderblock_pa_t_kernel(
         regroup_weight(2, 0)
         regroup_weight(2, 1)
 
-        sched = {}
+        plan = {}
 
-        def put(step, name, fn, *a):
-            sched.setdefault((step, name), []).append((fn, a))
+        def put(step, stage_name, work, *arguments):
+            plan.setdefault((step, stage_name), []).append((work, arguments))
 
-        for s in range(PER_GROUP, STEPS):
-            g = s // PER_GROUP
-            if g == 1:
-                st = math.floor(G1_BASE + (s - PER_GROUP) / G1_RATE)
-            else:
-                st = s - LS_LATE
-            put(st, 'stats', statistics, s)
-            put(st + AGG, 'aggr', aggregate, s)
-            if s % TILES in s_tiles(g):
-                put(st + 1, 'second', s_second, s)
-            if s % TILES == TILES - 1:
-                first = s - TILES + 1
-                d = st + DEV
-                put(d, 'dev', deviation, first)
-                put(d, 'off', offsets, first)
-                for i in range(TILES):
-                    put(d + i // 2, 'scale', scale, first + i)
-        for q in range(PAIRS // GROUPS, PAIRS):
-            one = q < 2 * PAIRS // GROUPS
-            put(math.floor(XT_BASE + (q - 6) / XT_RATE) if one else 2 * q - LEAD_XT, 'xt', transpose_x, q)
-            put(math.floor(Q_BASE + (q - 6) / Q_RATE) if one else 2 * q - LEAD_QUANTISE, 'quant', quantise_x, q)
-        for q in range(12, PAIRS):
-            put(2 * q - LEAD_XT - PL, 'perm', permute_x, q)
-        for u in range(STEPS):
-            put(FILLS.get(u, u - LEAD_FILL), 'fill', fill_nt, u)
-            put(SEEDS.get(u, u - LEAD_SEED), 'seed', seed, u)
+        for tile in range(PER_GROUP, STEPS):
+            g, l, i = split_tile(tile)
+            step = tile - (LEAD_STATISTICS_1 if g == 1 else LEAD_STATISTICS)
+            put(step, "statistics", statistics, tile)
+            put(step + 1, "spread", spread, tile)
+            if i == TILES - 1:
+                step += NORM_AFTER
+                put(step, "deviation", deviation, g, l)
+                put(step, "offsets", offsets, g, l)
+                for n in range(TILES):
+                    put(step + n // 2, "normalise", normalise, g, l, n)
+        for pair in range(PAIRS // GROUPS, PAIRS):
+            second = pair < 2 * PAIRS // GROUPS
+            put(2 * pair - (LEAD_X_1 if second else LEAD_X), "transposes", transpose_x, pair)
+            put(2 * pair - (LEAD_QUANTISE_1 if second else LEAD_QUANTISE), "quantise", quantise_x, pair)
+        for unit in range(STEPS):
+            put(nt_step(unit), "normed", transpose_normed, unit)
+            put(seed_step(unit), "seed", seed, unit)
+            put(unit + LAG_BACK, "back", back, unit)
+        for step in range(STEPS):
+            put(step, "products", products, step)
+        put(-4, "weights", quantise_weight, 2)
 
-        put(WV_AT, 'wv', quantise_weight, 2)
-
-        def do(step, name):
-            for fn, a in sched.pop((step, name), []):
-                fn(*a)
-
-        for u in range(min(k[0] for k in sched), STEPS + LAG_BACK):
-            live = 0 <= u < STEPS
-            if live:
-                base, l = u - u % 3, u % 3
-                order = sorted(range(KINDS), key=lambda t: ORD[0] if on_scalar(base + t, l) else t)
-                for t in order:
-                    product(base + t, l)
-            do(u, 'quant')
-            do(u, 'stats')
-            do(u, 'aggr')
-            do(u, 'second')
-            do(u, 'seed')
-            do(u, 'perm')
-            back(u - LAG_BACK)
-            do(u, 'fill')
-            do(u, 'xt')
-            do(u, 'wv')
-            do(u, 'dev')
-            do(u, 'off')
-            do(u, 'scale')
-        assert not sched, sorted(sched)
+        order = (
+            "products", "quantise", "statistics", "spread", "seed", "back",
+            "normed", "transposes", "weights", "deviation", "offsets", "normalise",
+        )
+        for step in range(PER_GROUP - LEAD_STATISTICS_1, STEPS + LAG_BACK):
+            for stage_name in order:
+                for work, arguments in plan.get((step, stage_name), []):
+                    work(*arguments)

from contextlib import ExitStack

import concourse.mybir as mybir
from concourse.masks import make_identity

F32 = mybir.dt.float32
BF16 = mybir.dt.bfloat16
U32 = mybir.dt.uint32
U8 = mybir.dt.uint8
FP8X4 = mybir.dt.float8_e4m3fn_x4
ALU = mybir.AluOpType
ACT = mybir.ActivationFunctionType

BATCH, LAYERS, SEQ, D = 2, 3, 1024, 512
EPS = 1e-5
P = 128
PACK = 4
MX_ALIGN = 256
TILES = 4
HALVES = SEQ // (P * TILES)
GROUPS = BATCH * HALVES
BLOCKS = D // P
KINDS = 3
PER_GROUP = BLOCKS * LAYERS
STEPS = GROUPS * PER_GROUP
PAIRS = STEPS // 2

VECTOR_TILES = 2

LEAD_STATISTICS = 22
LEAD_STATISTICS_1 = 19
NORM_AFTER = 2
LEAD_X = 16
LEAD_X_1 = 13
LEAD_QUANTISE = 12
LEAD_QUANTISE_1 = 11
LEAD_NT = 6
LEAD_SEED = 3
LAG_BACK = 3

FLOPS = 2 * BATCH * LAYERS * SEQ * D * KINDS * D


def nt_step(unit):
    block, third = divmod(unit, KINDS)
    if block == 0:
        return -3
    if block == 1:
        return 0
    if block == BLOCKS:
        return PER_GROUP - 4 + min(third, 1)
    return unit - LEAD_NT


def seed_step(unit):
    block, kind = divmod(unit, KINDS)
    if block == 0:
        return -2
    if block == 1:
        return 1 + kind // 2
    if block == BLOCKS:
        return PER_GROUP - 2 + kind // 2
    return unit - LEAD_SEED


def tile_dcadecoderblock_pa_t_kernel(
    tc,
    layer_outputs,
    grn_q_W, grn_q_b, grn_q_g, grn_q_be,
    grn_k_W, grn_k_b, grn_k_g, grn_k_be,
    grn_v_W, grn_v_b, grn_v_g, grn_v_be,
    out_0, out_1, out_2,
):
    nc = tc.nc
    weights = [grn_q_W, grn_k_W, grn_v_W]
    vectors = [grn_q_b, grn_q_g, grn_q_be, grn_k_b, grn_k_g, grn_k_be, grn_v_b, grn_v_g, grn_v_be]
    outs = [out_0, out_1, out_2]

    with ExitStack() as stack:
        stack.enter_context(tc.manual_schedule())
        keep = stack.enter_context(tc.tile_pool(name="keep", bufs=1))
        stage = stack.enter_context(tc.tile_pool(name="stage", bufs=2))
        small = stack.enter_context(tc.tile_pool(name="small", bufs=4))
        psum = stack.enter_context(tc.psum_pool(name="psum", bufs=2))

        def rows_of_group(dram, g):
            return dram[g // HALVES].rearrange("(p h i) f -> p h i f", h=HALVES, i=TILES)[:, g % HALVES]

        x_sb = {}

        def load_x(g, l):
            x_sb[(g, l)] = keep.tile([P, TILES, D], BF16, name="x%d_%d" % (g, l))
            nc.sync.dma_start(out=x_sb[(g, l)][:], in_=rows_of_group(layer_outputs[:, l], g))

        w_raw = {}

        def load_weight(t):
            w_raw[t] = keep.tile([P, PACK, D], BF16, name="w_raw%d" % t)
            nc.sync.dma_start(out=w_raw[t][:], in_=weights[t].rearrange("(p j) c -> p j c", j=PACK))

        for n in range(LAYERS):
            load_x(0, n)
            load_weight(n)
        vec_rows = keep.tile([P, P], BF16, name="vec_rows")
        nc.vector.memset(vec_rows[:], 0.0)
        for n, vec in enumerate(vectors):
            nc.sync.dma_start(
                out=vec_rows[BLOCKS * n : BLOCKS * n + BLOCKS, :],
                in_=vec.rearrange("(j p) -> j p", p=P),
            )
        for g in range(1, GROUPS):
            for l in range(LAYERS):
                load_x(g, l)

        ident_f = keep.tile([P, P], F32, name="ident_f")
        make_identity(nc, ident_f[:])
        ident_b = keep.tile([P, P], BF16, name="ident_b")
        make_identity(nc, ident_b[:])
        eps = keep.tile([P, 1], F32, name="eps")
        nc.vector.memset(eps[:], EPS)

        vec_cols = keep.tile([P, KINDS, 3, BLOCKS], F32, name="vec_cols")
        bias = vec_cols[:, :, 0, :]
        gain = vec_cols[:, :, 1, :]
        shift = vec_cols[:, :, 2, :]
        neg_bias = keep.tile([P, KINDS, BLOCKS], F32, name="neg_bias")
        bias_shift = keep.tile([P, KINDS, BLOCKS], F32, name="bias_shift")
        rest = keep.tile([P, KINDS, BLOCKS], F32, name="rest")

        def split_unit(unit):
            g, within = divmod(unit, PER_GROUP)
            j, t = divmod(within, KINDS)
            return g, j, t

        def split_tile(tile):
            g, within = divmod(tile, PER_GROUP)
            l, i = divmod(within, TILES)
            return g, l, i

        def constants():
            vec_ps = psum.tile([P, P], BF16, tag="nt", name="vec_ps")
            nc.tensor.transpose(vec_ps[:], vec_rows[:], ident_b[:])
            nc.scalar.copy(
                out=vec_cols[:].rearrange("p t v j -> p (t v j)"), in_=vec_ps[:, 0 : KINDS * 3 * BLOCKS]
            )
            nc.gpsimd.tensor_scalar(
                out=neg_bias[:], in0=bias, scalar1=-1.0, scalar2=0.0, op0=ALU.mult, op1=ALU.add
            )
            nc.gpsimd.tensor_tensor(out=bias_shift[:], in0=bias, in1=shift, op=ALU.add)
            nc.gpsimd.tensor_scalar(
                out=rest[:], in0=bias_shift[:], scalar1=float(LAYERS), scalar2=0.0, op0=ALU.mult, op1=ALU.add
            )

        w_grouped = {}
        w_codes = {}
        w_scales = {}

        def grouped_weight(t):
            w_grouped[t] = stage.tile([P, D, PACK], BF16, align_bytes=MX_ALIGN, bufs=KINDS, name="w_grouped")

        def regroup_weight(t, half):
            if half == 0:
                grouped_weight(t)
            cols = slice(D // 2 * half, D // 2 * half + D // 2)
            nc.scalar.copy(
                out=w_grouped[t][:, cols, :].rearrange("p (c i) t -> p c t i", i=4),
                in_=w_raw[t][:, :, cols].rearrange("p t (c i) -> p c t i", i=4),
            )

        def quantise_weight(t):
            w_codes[t] = keep.tile([P, D], U32, align_bytes=MX_ALIGN, name="w_codes%d" % t)
            w_scales[t] = keep.tile([P, D], U8, align_bytes=MX_ALIGN, name="w_scales%d" % t)
            nc.vector.quantize_mx(
                out=w_codes[t][:].bitcast(FP8X4),
                scales=w_scales[t][:],
                in_=w_grouped[t][:].rearrange("p c t -> p (c t)"),
            )

        x_grouped = {}
        x_codes = {}
        x_scales = {}

        def transpose_x(pair):
            g, l, i = split_tile(2 * pair)
            words = x_sb[(g, l)][:].bitcast(F32)
            xt = psum.tile([P, 2, 2, P], F32, tag="back", name="xt")
            for n in range(2):
                for u in range(2):
                    nc.tensor.transpose(xt[:, n, u, :], words[:, i + n, u : 2 * P : 2], ident_f[:])
            x_grouped[pair] = stage.tile([P, 2, P, PACK], BF16, align_bytes=MX_ALIGN, bufs=4, name="x_grouped")
            nc.scalar.copy(
                out=x_grouped[pair][:].rearrange("p n r t -> p (n r t)").bitcast(F32)
                .rearrange("p (n r u) -> p n r u", n=2, u=2),
                in_=xt[:].rearrange("p n u r -> p n r u"),
            )

        def quantise_x(pair):
            g, l, i = split_tile(2 * pair)
            if i == 0:
                x_codes[(g, l)] = stage.tile(
                    [P, TILES * P], U32, align_bytes=MX_ALIGN, bufs=2 * LAYERS, name="x_codes"
                )
                x_scales[(g, l)] = stage.tile(
                    [P, TILES * P], U8, align_bytes=MX_ALIGN, bufs=2 * LAYERS, name="x_scales"
                )
            nc.vector.quantize_mx(
                out=x_codes[(g, l)][:, P * i : P * i + 2 * P].bitcast(FP8X4),
                scales=x_scales[(g, l)][:, P * i : P * i + 2 * P],
                in_=x_grouped[pair][:].rearrange("p n r t -> p (n r t)"),
            )

        stats = {}
        mean_var = {}
        squares = {}
        rstd = {}
        neg_rstd = {}
        offset = {}
        normed = {}

        def vector_tiles(g):
            return TILES if g == 0 else VECTOR_TILES

        def statistics(tile):
            g, l, i = split_tile(tile)
            if i == 0:
                stats[(g, l)] = small.tile([P, TILES, 6], F32, name="stats")
            if i < vector_tiles(g):
                nc.vector.bn_stats(out=stats[(g, l)][:, i, :], in_=x_sb[(g, l)][:, i, :])
            else:
                junk = stage.tile([P, D], BF16, name="junk")
                nc.scalar.activation(
                    out=junk[:], in_=x_sb[(g, l)][:, i, :], func=ACT.Identity, bias=0.0, scale=1.0 / D,
                    accum_out=mean_var[(g, l)][:, i, 0:1],
                )

        def spread(tile):
            g, l, i = split_tile(tile)
            if i == 0:
                mean_var[(g, l)] = small.tile([P, TILES, 2], F32, name="mean_var")
            if i < vector_tiles(g):
                nc.vector.bn_aggr(out=mean_var[(g, l)][:, i, :], in_=stats[(g, l)][:, i, :])
            else:
                junk = stage.tile([P, D], BF16, name="junk")
                if i == vector_tiles(g):
                    squares[(g, l)] = small.tile([P, TILES], F32, name="squares")
                nc.scalar.activation(
                    out=junk[:], in_=x_sb[(g, l)][:, i, :], func=ACT.Square, scale=-1.0,
                    bias=mean_var[(g, l)][:, i, 0:1], accum_out=squares[(g, l)][:, i : i + 1],
                )

        def deviation(g, l):
            rstd[(g, l)] = small.tile([P, TILES], F32, name="rstd")
            neg_rstd[(g, l)] = small.tile([P, TILES], F32, name="neg_rstd")
            n = vector_tiles(g)
            nc.scalar.activation(
                out=rstd[(g, l)][:, :n], in_=mean_var[(g, l)][:, :n, 1],
                func=ACT.Abs_reciprocal_sqrt, bias=eps[:], scale=1.0,
            )
            if n < TILES:
                nc.scalar.activation(
                    out=rstd[(g, l)][:, n:], in_=squares[(g, l)][:, n:],
                    func=ACT.Abs_reciprocal_sqrt, bias=eps[:], scale=1.0 / D,
                )
            nc.scalar.mul(out=neg_rstd[(g, l)][:], in_=rstd[(g, l)][:], mul=-1.0)

        def offsets(g, l):
            offset[(g, l)] = small.tile([P, TILES], F32, name="offset")
            nc.gpsimd.tensor_tensor(
                out=offset[(g, l)][:], in0=mean_var[(g, l)][:, :, 0], in1=neg_rstd[(g, l)][:], op=ALU.mult
            )

        def normalise(g, l, i):
            y = stage.tile([P, D], F32, bufs=2 * PER_GROUP, name="normed")
            engine = nc.vector if g == 0 and l > 0 else nc.gpsimd
            engine.tensor_scalar(
                out=y[:], in0=x_sb[(g, l)][:, i, :],
                scalar1=rstd[(g, l)][:, i : i + 1], scalar2=offset[(g, l)][:, i : i + 1],
                op0=ALU.mult, op1=ALU.add,
            )
            normed[(g, l, i)] = y

        nt = {}
        acc = {}

        def transpose_normed(unit):
            g, j, third = split_unit(unit)
            if third == 0:
                nt[(g, j)] = psum.tile([P, TILES * P], F32, tag="nt", name="nt")
            for n in range(TILES * third, TILES * third + TILES):
                i, l = divmod(n, LAYERS)
                nc.tensor.matmul(
                    out=nt[(g, j)][:, P * i : P * i + P],
                    lhsT=normed[(g, l, i)][:, P * j : P * j + P],
                    rhs=ident_f[:],
                    is_transpose=True,
                    start=(l == 0),
                    stop=(l == LAYERS - 1),
                )

        def seed(unit):
            g, j, t = split_unit(unit)
            acc[unit] = stage.tile([P, TILES * P], F32, bufs=12, name="acc")
            nc.scalar.activation(
                out=acc[unit][:], in_=nt[(g, j)][:], func=ACT.Identity,
                scale=gain[:, t, j : j + 1], bias=rest[:, t, j : j + 1],
            )

        def products(step):
            g, j, l = split_unit(step)
            cols = slice(P * j, P * j + P)
            for t in range(KINDS):
                unit = step - l + t
                prod = psum.tile([P, TILES * P], F32, tag="prod", bufs=4, name="prod")
                nc.tensor.matmul_mx(
                    out=prod[:],
                    lhsT=w_codes[t][:, cols].bitcast(FP8X4),
                    lhsT_scale=w_scales[t][:, cols],
                    rhs=x_codes[(g, l)][:].bitcast(FP8X4),
                    rhs_scale=x_scales[(g, l)][:],
                    start=True,
                    stop=True,
                )
                nc.vector.scalar_tensor_tensor(
                    out=acc[unit][:], in0=prod[:], scalar=neg_bias[:, t, j : j + 1],
                    in1=acc[unit][:], op0=ALU.max, op1=ALU.add,
                )

        def back(unit):
            g, j, t = split_unit(unit)
            turned = psum.tile([P, TILES, P], F32, tag="back", name="turned")
            for i in range(TILES):
                nc.tensor.transpose(turned[:, i, :], acc[unit][:, P * i : P * i + P], ident_f[:])
            result = stage.tile([P, TILES, P], F32, bufs=4, name="result")
            nc.scalar.copy(out=result[:], in_=turned[:])
            nc.sync.dma_start(out=rows_of_group(outs[t], g)[:, :, P * j : P * j + P], in_=result[:])

        warm = small.tile([P, 1], F32, name="warm")
        nc.scalar.activation(out=warm[:], in_=eps[:], func=ACT.Abs_reciprocal_sqrt, bias=eps[:], scale=1.0)

        def layer_statistics(l):
            first = TILES * l
            for tile in range(first, first + TILES):
                statistics(tile)
                if tile > first:
                    spread(tile - 1)
            spread(first + TILES - 1)

        def layer_norm(l):
            offsets(0, l)
            for i in range(TILES):
                normalise(0, l, i)

        def layer_transposes(l):
            for pair in (2 * l, 2 * l + 1):
                transpose_x(pair)

        def layer_quantise(l):
            for pair in (2 * l, 2 * l + 1):
                quantise_x(pair)

        layer_statistics(0)
        layer_transposes(0)
        regroup_weight(0, 0)
        deviation(0, 0)
        layer_statistics(1)
        layer_norm(0)
        regroup_weight(0, 1)
        layer_transposes(1)
        layer_quantise(0)
        deviation(0, 1)
        regroup_weight(1, 0)
        layer_statistics(2)
        layer_norm(1)
        layer_quantise(1)
        quantise_weight(0)
        regroup_weight(1, 1)
        layer_transposes(2)
        deviation(0, 2)
        layer_norm(2)
        constants()
        layer_quantise(2)
        quantise_weight(1)
        regroup_weight(2, 0)
        regroup_weight(2, 1)

        plan = {}

        def put(step, stage_name, work, *arguments):
            plan.setdefault((step, stage_name), []).append((work, arguments))

        for tile in range(PER_GROUP, STEPS):
            g, l, i = split_tile(tile)
            step = tile - (LEAD_STATISTICS_1 if g == 1 else LEAD_STATISTICS)
            put(step, "statistics", statistics, tile)
            put(step + 1, "spread", spread, tile)
            if i == TILES - 1:
                step += NORM_AFTER
                put(step, "deviation", deviation, g, l)
                put(step, "offsets", offsets, g, l)
                for n in range(TILES):
                    put(step + n // 2, "normalise", normalise, g, l, n)
        for pair in range(PAIRS // GROUPS, PAIRS):
            second = pair < 2 * PAIRS // GROUPS
            put(2 * pair - (LEAD_X_1 if second else LEAD_X), "transposes", transpose_x, pair)
            put(2 * pair - (LEAD_QUANTISE_1 if second else LEAD_QUANTISE), "quantise", quantise_x, pair)
        for unit in range(STEPS):
            put(nt_step(unit), "normed", transpose_normed, unit)
            put(seed_step(unit), "seed", seed, unit)
            put(unit + LAG_BACK, "back", back, unit)
        for step in range(STEPS):
            put(step, "products", products, step)
        put(-4, "weights", quantise_weight, 2)

        order = (
            "products", "quantise", "statistics", "spread", "seed", "back",
            "normed", "transposes", "weights", "deviation", "offsets", "normalise",
        )
        for step in range(PER_GROUP - LEAD_STATISTICS_1, STEPS + LAG_BACK):
            for stage_name in order:
                for work, arguments in plan.get((step, stage_name), []):
                    work(*arguments)
